import numpy as np
import ml_dtypes


def mxq(x, axis, fmt="e4m3"):
    dtype, down = {"e4m3": (ml_dtypes.float8_e4m3fn, 7), "e5m2": (ml_dtypes.float8_e5m2, 14)}[fmt]
    v = np.moveaxis(np.asarray(x, np.float32).astype(ml_dtypes.bfloat16).astype(np.float64), axis, -1)
    blocks = v.reshape(v.shape[:-1] + (-1, 32))
    amax = np.abs(blocks).max(-1, keepdims=True)
    byte = np.maximum(np.where(amax > 0, np.frexp(amax)[1] - 1 + 127, 0) - down, 1)
    scale = np.exp2(byte - 127.0)
    codes = (blocks / scale).astype(np.float32).astype(dtype).astype(np.float64)
    return np.moveaxis((codes * scale).reshape(v.shape), -1, axis)


WIDE = False


def mx_kscale(k):
    if not WIDE:
        return np.ones(k)
    levels = np.array([10, -10, 5, -5, 0])
    a = np.random.permutation(np.resize(levels, k // 512 * 4)).reshape(k // 512, 4)
    idx = np.arange(k)
    return np.exp2(a[idx // 512, idx % 128 // 32])


BF16 = ml_dtypes.bfloat16


def bf(x):
    return np.asarray(x, np.float32).astype(BF16)


def f64(x):
    return np.asarray(x).astype(np.float64)


B, D, S, O = 8192, 512, 512, 256
K1 = D + S
P = S // 2
EPS = 1e-6


def sigmoid(v):
    return 1.0 / (1.0 + np.exp(-v))


def setup_inputs():
    r = np.random.standard_normal
    s = np.concatenate([mx_kscale(D), np.ones(S)])
    t = mx_kscale(S)
    return {
        "inputs": bf(r((B, D)) * s[:D]),
        "states": bf(r((B, S))),
        "W1": bf(r((K1, S)) / np.sqrt(K1) / s[:, None] * t),
        "b1": bf(r(S) * 0.2 * t),
        "W2": bf(r((S, P)) / np.sqrt(S) / t[:, None]),
        "b2": bf(r(P) * 0.2),
        "excitatory_potential": bf(1.0 + 0.1 * r(S)),
        "inhibitory_potential": bf(-1.0 + 0.1 * r(S)),
        "capacitance": bf(1.0 + 0.1 * r(S)),
        "max_conductance": bf(1.0 + 0.1 * r((S, 2))),
        "mean_conductance_potential": bf(0.3 * r((S, 2))),
        "std_conductance": bf(1.0 + 0.2 * r((S, 2))),
        "gamma": bf(1.0 + 0.1 * r(S)),
        "beta": bf(0.1 * r(S)),
    }


def reference(inputs, states, W1, b1, W2, b2, excitatory_potential, inhibitory_potential, capacitance,
              max_conductance, mean_conductance_potential, std_conductance, gamma, beta):
    v = f64(states)
    b, s = v.shape
    intervals = np.ones((b, 1))
    cat = np.concatenate([f64(inputs), v], -1)
    h = (mxq(cat, 1, "e4m3") @ mxq(f64(W1), 0, "e4m3")) + f64(b1)
    pre = (mxq(h, 1, "e4m3") @ mxq(f64(W2), 0, "e4m3")) + f64(b2)
    memory_cell_inputs = np.stack([pre, -pre], -1).reshape(b, s)
    pairs = v.reshape(b, s // 2, 2)
    rolled = np.roll(pairs, 1, axis=-1)
    presyn = np.concatenate([pairs, rolled], -1).reshape(b, s, 2)
    g = f64(max_conductance) * sigmoid(f64(std_conductance) * (presyn - f64(mean_conductance_potential)))
    rev = np.stack([f64(excitatory_potential), f64(inhibitory_potential)], -1)
    diff = rev - v[..., None]
    states_change = (memory_cell_inputs + np.sum(g * diff, -1)) / f64(capacitance) * intervals
    x = v + states_change
    mu = np.mean(x, -1, keepdims=True)
    var = np.mean((x - mu) ** 2, -1, keepdims=True)
    return (x - mu) * (1.0 / np.sqrt(var + EPS)) * f64(gamma) + f64(beta)

@@ -1,0 +1,296 @@
+from contextlib import ExitStack
+
+import concourse.mybir as mybir
+from concourse.masks import make_identity
+
+F32 = mybir.dt.float32
+BF16 = mybir.dt.bfloat16
+U32 = mybir.dt.uint32
+U8 = mybir.dt.uint8
+FP8X4 = mybir.dt.float8_e4m3fn_x4
+ALU = mybir.AluOpType
+ACT = mybir.ActivationFunctionType
+
+P = 128
+PACK = 4
+B, D, S = 8192, 512, 512
+PAIRS = S // 2
+EPS = 1e-6
+ROW_TILES = 4
+BLOCK = ROW_TILES * P
+N_BLOCKS = B // BLOCK
+PLANES = 4
+
+FLOPS = 2 * B * ((D + S) * S + S * PAIRS)
+
+
+def load_cell_constants(nc, pool, vectors, tables, b1, b2):
+    slot = 16
+    raw = pool.tile([P, 8, slot], BF16)
+    nc.vector.memset(raw[:], 0.0)
+    with nc.allow_non_contiguous_dma(reason="per-cell constants, a few bytes a partition, loaded once"):
+        for i, vec in enumerate(vectors):
+            nc.scalar.dma_start(
+                out=raw[:, i, 0:PLANES].rearrange("p (u e) -> p u e", u=2),
+                in_=vec.rearrange("(u p e) -> p u e", u=2, p=P),
+            )
+        for i, tab in enumerate(tables):
+            nc.scalar.dma_start(
+                out=raw[:, 3 + i, 0 : 2 * PLANES].rearrange("p (u k) -> p u k", u=2),
+                in_=tab.rearrange("(u p e) c -> p u (e c)", u=2, p=P),
+            )
+        nc.scalar.dma_start(out=raw[:, 6, 0:2], in_=b2.rearrange("(u p) -> p u", p=P))
+        nc.scalar.dma_start(out=raw[:, 7, 0:PACK], in_=b1.rearrange("(m t) -> m t", t=PACK))
+    par = pool.tile([P, 8, slot], F32)
+    nc.vector.tensor_copy(out=par[:], in_=raw[:])
+    return par
+
+
+def tile_memorylayercell_pa_t_kernel(
+    tc,
+    inputs,
+    states,
+    W1,
+    b1,
+    W2,
+    b2,
+    excitatory_potential,
+    inhibitory_potential,
+    capacitance,
+    max_conductance,
+    mean_conductance_potential,
+    std_conductance,
+    gamma,
+    beta,
+    out,
+):
+    nc = tc.nc
+    with ExitStack() as stack:
+        consts = stack.enter_context(tc.tile_pool(name="consts", bufs=1))
+        rows_in = stack.enter_context(tc.tile_pool(name="rows_in", bufs=3))
+        work = stack.enter_context(tc.tile_pool(name="work", bufs=2))
+        psum = stack.enter_context(tc.psum_pool(name="psum", bufs=2))
+
+        def load_block(b):
+            rows = slice(b * BLOCK, (b + 1) * BLOCK)
+            in_sb = rows_in.tile([P, ROW_TILES * D], BF16)
+            nc.sync.dma_start(out=in_sb[:], in_=inputs[rows, :].rearrange("(p a) d -> p (a d)", a=ROW_TILES))
+            st_sb = rows_in.tile([P, ROW_TILES * S], BF16)
+            nc.sync.dma_start(out=st_sb[:], in_=states[rows, :].rearrange("(p a) d -> p (a d)", a=ROW_TILES))
+            return in_sb, st_sb
+
+        first_block = load_block(0)
+
+        ident = consts.tile([P, P], F32)
+        make_identity(nc, ident[:])
+
+        w1_raw = consts.tile([P, 2, PACK, S], BF16)
+        nc.sync.dma_start(
+            out=w1_raw[:].rearrange("p g (u e) n -> p (g u) (e n)", u=2),
+            in_=W1.rearrange("(gu p e) n -> p gu (e n)", gu=4, p=P),
+        )
+        w2_raw = consts.tile([P, PACK, PAIRS], BF16)
+        nc.sync.dma_start(
+            out=w2_raw[:].rearrange("m t n -> m (t n)"),
+            in_=W2.rearrange("(m t) n -> m (t n)", t=PACK),
+        )
+        w1_grp = consts.tile([P, 2, S * PACK], BF16, align_bytes=64)
+        w1_codes = consts.tile([P, 2, S], U32, align_bytes=64)
+        w1_scales = consts.tile([P, 2, S], U8, align_bytes=64)
+        for g in range(2):
+            nc.vector.tensor_copy(
+                out=w1_grp[:, g, :].rearrange("p (c m t) -> p c m t", c=PACK, m=P),
+                in_=w1_raw[:, g, :, :].rearrange("p t (m c) -> p c m t", c=PACK),
+            )
+        w2_grp = consts.tile([P, PAIRS, PACK], BF16, align_bytes=64)
+        nc.vector.tensor_copy(out=w2_grp[:], in_=w2_raw[:].rearrange("m t n -> m n t"))
+        for g in range(2):
+            nc.vector.quantize_mx(
+                out=w1_codes[:, g, :].bitcast(FP8X4), scales=w1_scales[:, g, :], in_=w1_grp[:, g, :]
+            )
+        w2_codes = consts.tile([P, PAIRS], U32, align_bytes=64)
+        w2_scales = consts.tile([P, PAIRS], U8, align_bytes=64)
+        nc.vector.quantize_mx(
+            out=w2_codes[:].bitcast(FP8X4), scales=w2_scales[:], in_=w2_grp[:].rearrange("m n t -> m (n t)")
+        )
+
+        par = load_cell_constants(
+            nc,
+            consts,
+            [excitatory_potential, inhibitory_potential, capacitance],
+            [max_conductance, mean_conductance_potential, std_conductance],
+            b1,
+            b2,
+        )
+        reversal = [par[:, 0, 0:PLANES], par[:, 1, 0:PLANES]]
+        b1_col = par[:, 7, 0:PACK]
+        inv_cap = consts.tile([P, PLANES], F32)
+        nc.vector.reciprocal(out=inv_cap[:], in_=par[:, 2, 0:PLANES])
+        slope = []
+        shift = []
+        neg_gain = []
+        for k in range(2):
+            slope_k = consts.tile([P, PLANES], F32, name="slope%d" % k)
+            nc.vector.tensor_copy(out=slope_k[:], in_=par[:, 5, k : 2 * PLANES : 2])
+            shift_k = consts.tile([P, PLANES], F32, name="shift%d" % k)
+            nc.vector.scalar_tensor_tensor(
+                out=shift_k[:], in0=slope_k[:], scalar=-1.0, in1=par[:, 4, k : 2 * PLANES : 2],
+                op0=ALU.mult, op1=ALU.mult,
+            )
+            neg_gain_k = consts.tile([P, PLANES], F32, name="neg_gain%d" % k)
+            nc.vector.scalar_tensor_tensor(
+                out=neg_gain_k[:], in0=par[:, 3, k : 2 * PLANES : 2], scalar=-1.0, in1=inv_cap[:],
+                op0=ALU.mult, op1=ALU.mult,
+            )
+            slope.append(slope_k)
+            shift.append(shift_k)
+            neg_gain.append(neg_gain_k)
+        gate_offset = consts.tile([P, 2], F32)
+        nc.vector.memset(gate_offset[:, 0:1], 1.0)
+        nc.vector.memset(gate_offset[:, 1:2], 0.0)
+        drive_scale = consts.tile([P, PLANES], F32)
+        nc.vector.tensor_copy(out=drive_scale[:, 0:PLANES:2], in_=inv_cap[:, 0:PLANES:2])
+        nc.vector.tensor_scalar_mul(out=drive_scale[:, 1:PLANES:2], in0=inv_cap[:, 1:PLANES:2], scalar1=-1.0)
+        drive_bias = consts.tile([P, PLANES], F32)
+        nc.vector.tensor_mul(
+            out=drive_bias[:].rearrange("p (u e) -> p u e", u=2),
+            in0=drive_scale[:].rearrange("p (u e) -> p u e", u=2),
+            in1=par[:, 6, 0:2].unsqueeze(2).to_broadcast([P, 2, 2]),
+        )
+        nc.vector.tensor_add(out=drive_bias[:], in0=drive_bias[:], in1=reversal[0])
+        neg_half = consts.tile([P, ROW_TILES], F32)
+        nc.vector.memset(neg_half[:], -0.5)
+        gamma_rows = consts.tile([P, S], BF16)
+        nc.scalar.dma_start(out=gamma_rows[:], in_=gamma.partition_broadcast(P))
+        beta_rows = consts.tile([P, S], BF16)
+        nc.scalar.dma_start(out=beta_rows[:], in_=beta.partition_broadcast(P))
+
+        for b in range(N_BLOCKS):
+            in_sb, st_sb = first_block if b == 0 else load_block(b)
+
+            cat_codes = work.tile([P, 2, BLOCK], U32, align_bytes=64)
+            cat_scales = work.tile([P, 2, BLOCK], U8, align_bytes=64)
+            in_grp = work.tile([P, BLOCK * PACK], BF16, align_bytes=64)
+            st_grp = work.tile([P, BLOCK * PACK], BF16, align_bytes=64)
+            for g, (src, grp) in enumerate(((in_sb, in_grp), (st_sb, st_grp))):
+                words = src[:].bitcast(F32).rearrange("p (a w) -> p a w", a=ROW_TILES)
+                grp_words = grp[:].bitcast(F32).rearrange("p (r u) -> p r u", u=2)
+                for half in range(2):
+                    cat_t = psum.tile([P, 2, 2 * P], F32)
+                    for u in range(2):
+                        for al in range(2):
+                            nc.tensor.transpose(
+                                out=cat_t[:, u, al * P : (al + 1) * P],
+                                in_=words[:, 2 * half + al, u * P : (u + 1) * P],
+                                identity=ident[:],
+                            )
+                    nc.scalar.copy(
+                        out=grp_words[:, half * 2 * P : (half + 1) * 2 * P, :],
+                        in_=cat_t[:].rearrange("p u r -> p r u"),
+                    )
+                nc.vector.quantize_mx(
+                    out=cat_codes[:, g, :].bitcast(FP8X4), scales=cat_scales[:, g, :], in_=grp[:]
+                )
+
+            h_grp = work.tile([P, BLOCK, PACK], BF16, align_bytes=64)
+            for a in range(ROW_TILES):
+                cols = slice(a * P, (a + 1) * P)
+                h_acc = psum.tile([P, PACK, P], F32)
+                for c in range(PACK):
+                    for g in range(2):
+                        nc.tensor.matmul_mx(
+                            out=h_acc[:, c, :],
+                            lhsT=w1_codes[:, g, c * P : (c + 1) * P].bitcast(FP8X4),
+                            lhsT_scale=w1_scales[:, g, c * P : (c + 1) * P],
+                            rhs=cat_codes[:, g, cols].bitcast(FP8X4),
+                            rhs_scale=cat_scales[:, g, cols],
+                            start=(g == 0),
+                            stop=(g == 1),
+                        )
+                nc.vector.tensor_tensor(
+                    out=h_grp[:, cols, :],
+                    in0=h_acc[:].rearrange("m c r -> m r c"),
+                    in1=b1_col.unsqueeze(1).to_broadcast([P, P, PACK]),
+                    op=ALU.add,
+                )
+            h_codes = work.tile([P, BLOCK], U32, align_bytes=64)
+            h_scales = work.tile([P, BLOCK], U8, align_bytes=64)
+            nc.vector.quantize_mx(
+                out=h_codes[:].bitcast(FP8X4), scales=h_scales[:], in_=h_grp[:].rearrange("m r c -> m (r c)")
+            )
+
+            v = st_grp[:].rearrange("p (r q) -> p r q", q=PLANES)
+            gate = work.tile([P, 2, PLANES, BLOCK], F32)
+            for q in range(PLANES):
+                for k in range(2):
+                    seen = q if k == 0 else q ^ 1
+                    nc.scalar.activation(
+                        out=gate[:, k, q, :], in_=v[:, :, seen], func=ACT.Sigmoid,
+                        scale=slope[k][:, q : q + 1], bias=shift[k][:, q : q + 1],
+                    )
+                    nc.gpsimd.tensor_scalar(
+                        out=gate[:, k, q, :], in0=gate[:, k, q, :],
+                        scalar1=neg_gain[k][:, q : q + 1], scalar2=gate_offset[:, k : k + 1],
+                        op0=ALU.mult, op1=ALU.add,
+                    )
+                    nc.vector.scalar_tensor_tensor(
+                        out=gate[:, k, q, :], in0=v[:, :, q], scalar=reversal[k][:, q : q + 1],
+                        in1=gate[:, k, q, :], op0=ALU.subtract, op1=ALU.mult,
+                    )
+            drive = work.tile([P, PLANES, BLOCK], F32)
+            for u in range(2):
+                pre_acc = psum.tile([P, BLOCK], F32)
+                nc.tensor.matmul_mx(
+                    out=pre_acc[:],
+                    lhsT=w2_codes[:, u * P : (u + 1) * P].bitcast(FP8X4),
+                    lhsT_scale=w2_scales[:, u * P : (u + 1) * P],
+                    rhs=h_codes[:].bitcast(FP8X4),
+                    rhs_scale=h_scales[:],
+                    start=True,
+                    stop=True,
+                )
+                for e in range(2):
+                    q = 2 * u + e
+                    nc.scalar.activation(
+                        out=drive[:, q, :], in_=pre_acc[:], func=ACT.Identity,
+                        scale=drive_scale[:, q : q + 1], bias=drive_bias[:, q : q + 1],
+                    )
+
+            mean_var = work.tile([P, ROW_TILES, 2], F32)
+            centred = work.tile([P, ROW_TILES, S], F32)
+            for a in range(ROW_TILES):
+                cols = slice(a * P, (a + 1) * P)
+                x_acc = psum.tile([P, S], F32)
+                for q in range(PLANES):
+                    terms = (gate[:, 0, q, cols], gate[:, 1, q, cols], drive[:, q, cols])
+                    for i, term in enumerate(terms):
+                        nc.tensor.matmul(
+                            out=x_acc[:, q * P : (q + 1) * P], lhsT=term, rhs=ident[:], is_transpose=True,
+                            start=(i == 0), stop=(i == len(terms) - 1),
+                        )
+                stats = work.tile([P, 6], F32)
+                nc.vector.bn_stats(out=stats[:], in_=x_acc[:])
+                nc.vector.bn_aggr(out=mean_var[:, a, :], in_=stats[:])
+                for u in range(2):
+                    cells = slice(u * 2 * P, (u + 1) * 2 * P)
+                    nc.vector.scalar_tensor_tensor(
+                        out=centred[:, a, cells].rearrange("r (j e) -> r j e", e=2),
+                        in0=x_acc[:, cells].rearrange("r (e j) -> r j e", e=2),
+                        scalar=mean_var[:, a, 0:1],
+                        in1=gamma_rows[:, cells].rearrange("r (j e) -> r j e", e=2),
+                        op0=ALU.subtract, op1=ALU.mult,
+                    )
+            var_eps = work.tile([P, ROW_TILES], F32)
+            nc.gpsimd.tensor_scalar_add(out=var_eps[:], in0=mean_var[:, :, 1], scalar1=EPS)
+            rstd = work.tile([P, ROW_TILES], F32)
+            nc.gpsimd.tensor_tensor(out=rstd[:], in0=var_eps[:], in1=neg_half[:], op=ALU.pow)
+            out_sb = work.tile([P, ROW_TILES, S], F32)
+            for a in range(ROW_TILES):
+                nc.vector.scalar_tensor_tensor(
+                    out=out_sb[:, a, :], in0=centred[:, a, :], scalar=rstd[:, a : a + 1], in1=beta_rows[:],
+                    op0=ALU.mult, op1=ALU.add,
+                )
+            nc.sync.dma_start(
+                out=out[b * BLOCK : (b + 1) * BLOCK, :].rearrange("(p a) c -> p (a c)", a=ROW_TILES),
+                in_=out_sb[:].rearrange("p a c -> p (a c)"),
+            )

@@ -228,10 +228,9 @@ def tile_memorylayercell_pa_t_kernel(
                         out=gate[:, k, q, :], in_=v[:, :, seen], func=ACT.Sigmoid,
                         scale=slope[k][:, q : q + 1], bias=shift[k][:, q : q + 1],
                     )
-                    nc.gpsimd.tensor_scalar(
-                        out=gate[:, k, q, :], in0=gate[:, k, q, :],
-                        scalar1=neg_gain[k][:, q : q + 1], scalar2=gate_offset[:, k : k + 1],
-                        op0=ALU.mult, op1=ALU.add,
+                    nc.scalar.activation(
+                        out=gate[:, k, q, :], in_=gate[:, k, q, :], func=ACT.Identity,
+                        scale=neg_gain[k][:, q : q + 1], bias=gate_offset[:, k : k + 1],
                     )
                     nc.vector.scalar_tensor_tensor(
                         out=gate[:, k, q, :], in0=v[:, :, q], scalar=reversal[k][:, q : q + 1],

@@ -75,7 +75,7 @@ def tile_memorylayercell_pa_t_kernel(
             rows = slice(b * BLOCK, (b + 1) * BLOCK)
             in_sb = rows_in.tile([P, ROW_TILES * D], BF16)
             nc.sync.dma_start(out=in_sb[:], in_=inputs[rows, :].rearrange("(p a) d -> p (a d)", a=ROW_TILES))
-            st_sb = rows_in.tile([P, ROW_TILES * S], BF16)
+            st_sb = rows_in.tile([P, ROW_TILES * S], BF16, bufs=4)
             nc.sync.dma_start(out=st_sb[:], in_=states[rows, :].rearrange("(p a) d -> p (a d)", a=ROW_TILES))
             return in_sb, st_sb
 
@@ -164,6 +164,13 @@ def tile_memorylayercell_pa_t_kernel(
         nc.scalar.dma_start(out=gamma_rows[:], in_=gamma.partition_broadcast(P))
         beta_rows = consts.tile([P, S], BF16)
         nc.scalar.dma_start(out=beta_rows[:], in_=beta.partition_broadcast(P))
+        gamma_planes = consts.tile([P, S], BF16)
+        nc.vector.tensor_copy(
+            out=gamma_planes[:].rearrange("r (u e j) -> r u e j", u=2, e=2),
+            in_=gamma_rows[:].rearrange("r (u j e) -> r u e j", u=2, e=2),
+        )
+        beta_f32 = consts.tile([P, S], F32)
+        nc.vector.tensor_copy(out=beta_f32[:], in_=beta_rows[:])
 
         for b in range(N_BLOCKS):
             in_sb, st_sb = first_block if b == 0 else load_block(b)
@@ -195,7 +202,7 @@ def tile_memorylayercell_pa_t_kernel(
             h_grp = work.tile([P, BLOCK, PACK], BF16, align_bytes=64)
             for a in range(ROW_TILES):
                 cols = slice(a * P, (a + 1) * P)
-                h_acc = psum.tile([P, PACK, P], F32)
+                h_acc = psum.tile([P, PACK, P], F32, tag="mx_acc")
                 for c in range(PACK):
                     for g in range(2):
                         nc.tensor.matmul_mx(
@@ -220,7 +227,7 @@ def tile_memorylayercell_pa_t_kernel(
             )
 
             v = st_grp[:].rearrange("p (r q) -> p r q", q=PLANES)
-            gate = work.tile([P, 2, PLANES, BLOCK], F32)
+            gate = work.tile([P, 2, PLANES, BLOCK], F32, bufs=3)
             for q in range(PLANES):
                 for k in range(2):
                     seen = q if k == 0 else q ^ 1
@@ -228,17 +235,34 @@ def tile_memorylayercell_pa_t_kernel(
                         out=gate[:, k, q, :], in_=v[:, :, seen], func=ACT.Sigmoid,
                         scale=slope[k][:, q : q + 1], bias=shift[k][:, q : q + 1],
                     )
-                    nc.scalar.activation(
-                        out=gate[:, k, q, :], in_=gate[:, k, q, :], func=ACT.Identity,
-                        scale=neg_gain[k][:, q : q + 1], bias=gate_offset[:, k : k + 1],
+                    nc.gpsimd.tensor_scalar(
+                        out=gate[:, k, q, :], in0=gate[:, k, q, :],
+                        scalar1=neg_gain[k][:, q : q + 1], scalar2=gate_offset[:, k : k + 1],
+                        op0=ALU.mult, op1=ALU.add,
                     )
-                    nc.vector.scalar_tensor_tensor(
-                        out=gate[:, k, q, :], in0=v[:, :, q], scalar=reversal[k][:, q : q + 1],
-                        in1=gate[:, k, q, :], op0=ALU.subtract, op1=ALU.mult,
-                    )
+
+            st_words = st_sb[:].bitcast(F32).rearrange("p (a w) -> p a w", a=ROW_TILES)
+            for half in range(2):
+                rows = slice(half * 2 * P, (half + 1) * 2 * P)
+                st_v = psum.tile([P, 2, 2 * P], F32)
+                for u in range(2):
+                    for al in range(2):
+                        nc.tensor.transpose(
+                            out=st_v[:, u, al * P : (al + 1) * P],
+                            in_=st_words[:, 2 * half + al, u * P : (u + 1) * P],
+                            identity=ident[:],
+                        )
+                v_psum = st_v[:].bitcast(BF16).rearrange("p u (r e) -> p u r e", e=2)
+                for q in range(PLANES):
+                    for k in range(2):
+                        nc.vector.scalar_tensor_tensor(
+                            out=gate[:, k, q, rows], in0=v_psum[:, q // 2, :, q % 2],
+                            scalar=reversal[k][:, q : q + 1], in1=gate[:, k, q, rows],
+                            op0=ALU.subtract, op1=ALU.mult,
+                        )
             drive = work.tile([P, PLANES, BLOCK], F32)
             for u in range(2):
-                pre_acc = psum.tile([P, BLOCK], F32)
+                pre_acc = psum.tile([P, BLOCK], F32, tag="mx_acc")
                 nc.tensor.matmul_mx(
                     out=pre_acc[:],
                     lhsT=w2_codes[:, u * P : (u + 1) * P].bitcast(FP8X4),
@@ -256,7 +280,7 @@ def tile_memorylayercell_pa_t_kernel(
                     )
 
             mean_var = work.tile([P, ROW_TILES, 2], F32)
-            centred = work.tile([P, ROW_TILES, S], F32)
+            centred = work.tile([P, ROW_TILES, S], F32, bufs=3)
             for a in range(ROW_TILES):
                 cols = slice(a * P, (a + 1) * P)
                 x_acc = psum.tile([P, S], F32)
@@ -270,25 +294,25 @@ def tile_memorylayercell_pa_t_kernel(
                 stats = work.tile([P, 6], F32)
                 nc.vector.bn_stats(out=stats[:], in_=x_acc[:])
                 nc.vector.bn_aggr(out=mean_var[:, a, :], in_=stats[:])
-                for u in range(2):
-                    cells = slice(u * 2 * P, (u + 1) * 2 * P)
-                    nc.vector.scalar_tensor_tensor(
-                        out=centred[:, a, cells].rearrange("r (j e) -> r j e", e=2),
-                        in0=x_acc[:, cells].rearrange("r (e j) -> r j e", e=2),
-                        scalar=mean_var[:, a, 0:1],
-                        in1=gamma_rows[:, cells].rearrange("r (j e) -> r j e", e=2),
-                        op0=ALU.subtract, op1=ALU.mult,
-                    )
+                nc.vector.scalar_tensor_tensor(
+                    out=centred[:, a, :], in0=x_acc[:], scalar=mean_var[:, a, 0:1], in1=gamma_planes[:],
+                    op0=ALU.subtract, op1=ALU.mult,
+                )
             var_eps = work.tile([P, ROW_TILES], F32)
             nc.gpsimd.tensor_scalar_add(out=var_eps[:], in0=mean_var[:, :, 1], scalar1=EPS)
             rstd = work.tile([P, ROW_TILES], F32)
             nc.gpsimd.tensor_tensor(out=rstd[:], in0=var_eps[:], in1=neg_half[:], op=ALU.pow)
-            out_sb = work.tile([P, ROW_TILES, S], F32)
+            out_sb = work.tile([P, ROW_TILES, S], F32, bufs=3)
             for a in range(ROW_TILES):
-                nc.vector.scalar_tensor_tensor(
-                    out=out_sb[:, a, :], in0=centred[:, a, :], scalar=rstd[:, a : a + 1], in1=beta_rows[:],
-                    op0=ALU.mult, op1=ALU.add,
+                nc.scalar.activation(
+                    out=out_sb[:, a, :].rearrange("r (u j e) -> r u j e", u=2, e=2),
+                    in_=centred[:, a, :].rearrange("r (u e j) -> r u j e", u=2, e=2),
+                    func=ACT.Identity, scale=rstd[:, a : a + 1],
                 )
+            nc.gpsimd.tensor_tensor(
+                out=out_sb[:], in0=out_sb[:], in1=beta_f32[:].unsqueeze(1).to_broadcast([P, ROW_TILES, S]),
+                op=ALU.add,
+            )
             nc.sync.dma_start(
                 out=out[b * BLOCK : (b + 1) * BLOCK, :].rearrange("(p a) c -> p (a c)", a=ROW_TILES),
                 in_=out_sb[:].rearrange("p a c -> p (a c)"),

@@ -18,6 +18,7 @@ PAIRS = S // 2
 EPS = 1e-6
 ROW_TILES = 4
 BLOCK = ROW_TILES * P
+HALF = BLOCK // 2
 N_BLOCKS = B // BLOCK
 PLANES = 4
 
@@ -41,9 +42,7 @@ def load_cell_constants(nc, pool, vectors, tables, b1, b2):
             )
         nc.scalar.dma_start(out=raw[:, 6, 0:2], in_=b2.rearrange("(u p) -> p u", p=P))
         nc.scalar.dma_start(out=raw[:, 7, 0:PACK], in_=b1.rearrange("(m t) -> m t", t=PACK))
-    par = pool.tile([P, 8, slot], F32)
-    nc.vector.tensor_copy(out=par[:], in_=raw[:])
-    return par
+    return raw
 
 
 def tile_memorylayercell_pa_t_kernel(
@@ -70,35 +69,50 @@ def tile_memorylayercell_pa_t_kernel(
         rows_in = stack.enter_context(tc.tile_pool(name="rows_in", bufs=3))
         work = stack.enter_context(tc.tile_pool(name="work", bufs=2))
         psum = stack.enter_context(tc.psum_pool(name="psum", bufs=2))
+        stack.enter_context(tc.manual_schedule())
+        held = {}
 
-        def load_block(b):
+        def load(b):
             rows = slice(b * BLOCK, (b + 1) * BLOCK)
             in_sb = rows_in.tile([P, ROW_TILES * D], BF16)
             nc.sync.dma_start(out=in_sb[:], in_=inputs[rows, :].rearrange("(p a) d -> p (a d)", a=ROW_TILES))
-            st_sb = rows_in.tile([P, ROW_TILES * S], BF16, bufs=4)
+            st_sb = rows_in.tile([P, ROW_TILES * S], BF16)
             nc.sync.dma_start(out=st_sb[:], in_=states[rows, :].rearrange("(p a) d -> p (a d)", a=ROW_TILES))
-            return in_sb, st_sb
-
-        first_block = load_block(0)
-
-        ident = consts.tile([P, P], F32)
-        make_identity(nc, ident[:])
+            held["in_sb", b] = in_sb
+            held["st_sb", b] = st_sb
 
         w1_raw = consts.tile([P, 2, PACK, S], BF16)
         nc.sync.dma_start(
             out=w1_raw[:].rearrange("p g (u e) n -> p (g u) (e n)", u=2),
             in_=W1.rearrange("(gu p e) n -> p gu (e n)", gu=4, p=P),
         )
+        load(0)
         w2_raw = consts.tile([P, PACK, PAIRS], BF16)
         nc.sync.dma_start(
             out=w2_raw[:].rearrange("m t n -> m (t n)"),
             in_=W2.rearrange("(m t) n -> m (t n)", t=PACK),
         )
+        raw = load_cell_constants(
+            nc,
+            consts,
+            [excitatory_potential, inhibitory_potential, capacitance],
+            [max_conductance, mean_conductance_potential, std_conductance],
+            b1,
+            b2,
+        )
+        gamma_rows = consts.tile([P, S], BF16)
+        nc.scalar.dma_start(out=gamma_rows[:], in_=gamma.partition_broadcast(P))
+        beta_rows = consts.tile([P, S], BF16)
+        nc.scalar.dma_start(out=beta_rows[:], in_=beta.partition_broadcast(P))
+
+        ident = consts.tile([P, P], F32)
+        make_identity(nc, ident[:])
+
         w1_grp = consts.tile([P, 2, S * PACK], BF16, align_bytes=64)
         w1_codes = consts.tile([P, 2, S], U32, align_bytes=64)
         w1_scales = consts.tile([P, 2, S], U8, align_bytes=64)
-        for g in range(2):
-            nc.vector.tensor_copy(
+        for g, copy in enumerate((nc.vector.tensor_copy, nc.scalar.copy)):
+            copy(
                 out=w1_grp[:, g, :].rearrange("p (c m t) -> p c m t", c=PACK, m=P),
                 in_=w1_raw[:, g, :, :].rearrange("p t (m c) -> p c m t", c=PACK),
             )
@@ -114,14 +128,8 @@ def tile_memorylayercell_pa_t_kernel(
             out=w2_codes[:].bitcast(FP8X4), scales=w2_scales[:], in_=w2_grp[:].rearrange("m n t -> m (n t)")
         )
 
-        par = load_cell_constants(
-            nc,
-            consts,
-            [excitatory_potential, inhibitory_potential, capacitance],
-            [max_conductance, mean_conductance_potential, std_conductance],
-            b1,
-            b2,
-        )
+        par = consts.tile([P, 8, 16], F32)
+        nc.vector.tensor_copy(out=par[:], in_=raw[:])
         reversal = [par[:, 0, 0:PLANES], par[:, 1, 0:PLANES]]
         b1_col = par[:, 7, 0:PACK]
         inv_cap = consts.tile([P, PLANES], F32)
@@ -160,10 +168,6 @@ def tile_memorylayercell_pa_t_kernel(
         nc.vector.tensor_add(out=drive_bias[:], in0=drive_bias[:], in1=reversal[0])
         neg_half = consts.tile([P, ROW_TILES], F32)
         nc.vector.memset(neg_half[:], -0.5)
-        gamma_rows = consts.tile([P, S], BF16)
-        nc.scalar.dma_start(out=gamma_rows[:], in_=gamma.partition_broadcast(P))
-        beta_rows = consts.tile([P, S], BF16)
-        nc.scalar.dma_start(out=beta_rows[:], in_=beta.partition_broadcast(P))
         gamma_planes = consts.tile([P, S], BF16)
         nc.vector.tensor_copy(
             out=gamma_planes[:].rearrange("r (u e j) -> r u e j", u=2, e=2),
@@ -172,33 +176,41 @@ def tile_memorylayercell_pa_t_kernel(
         beta_f32 = consts.tile([P, S], F32)
         nc.vector.tensor_copy(out=beta_f32[:], in_=beta_rows[:])
 
-        for b in range(N_BLOCKS):
-            in_sb, st_sb = first_block if b == 0 else load_block(b)
+        def transpose_words(dst, src_sb, half):
+            words = src_sb[:].bitcast(F32).rearrange("p (a w) -> p a w", a=ROW_TILES)
+            for u in range(2):
+                for al in range(2):
+                    nc.tensor.transpose(
+                        out=dst[:, u, al * P : (al + 1) * P],
+                        in_=words[:, 2 * half + al, u * P : (u + 1) * P],
+                        identity=ident[:],
+                    )
 
-            cat_codes = work.tile([P, 2, BLOCK], U32, align_bytes=64)
-            cat_scales = work.tile([P, 2, BLOCK], U8, align_bytes=64)
-            in_grp = work.tile([P, BLOCK * PACK], BF16, align_bytes=64)
-            st_grp = work.tile([P, BLOCK * PACK], BF16, align_bytes=64)
-            for g, (src, grp) in enumerate(((in_sb, in_grp), (st_sb, st_grp))):
-                words = src[:].bitcast(F32).rearrange("p (a w) -> p a w", a=ROW_TILES)
+        def transpose_cat(b):
+            for name in ("in", "st"):
+                grp = work.tile([P, BLOCK * PACK], BF16, align_bytes=64, name=name + "_grp")
+                held[name + "_grp", b] = grp
                 grp_words = grp[:].bitcast(F32).rearrange("p (r u) -> p r u", u=2)
                 for half in range(2):
-                    cat_t = psum.tile([P, 2, 2 * P], F32)
-                    for u in range(2):
-                        for al in range(2):
-                            nc.tensor.transpose(
-                                out=cat_t[:, u, al * P : (al + 1) * P],
-                                in_=words[:, 2 * half + al, u * P : (u + 1) * P],
-                                identity=ident[:],
-                            )
+                    cat_t = psum.tile([P, 2, HALF], F32)
+                    transpose_words(cat_t, held[name + "_sb", b], half)
                     nc.scalar.copy(
-                        out=grp_words[:, half * 2 * P : (half + 1) * 2 * P, :],
+                        out=grp_words[:, half * HALF : (half + 1) * HALF, :],
                         in_=cat_t[:].rearrange("p u r -> p r u"),
                     )
-                nc.vector.quantize_mx(
-                    out=cat_codes[:, g, :].bitcast(FP8X4), scales=cat_scales[:, g, :], in_=grp[:]
-                )
 
+        def quantise_cat(b):
+            cat_codes = work.tile([P, 2, BLOCK], U32, align_bytes=64)
+            cat_scales = work.tile([P, 2, BLOCK], U8, align_bytes=64)
+            for g, name in enumerate(("in_grp", "st_grp")):
+                nc.vector.quantize_mx(
+                    out=cat_codes[:, g, :].bitcast(FP8X4), scales=cat_scales[:, g, :], in_=held[name, b][:]
+                )
+            held["cat_codes", b] = cat_codes
+            held["cat_scales", b] = cat_scales
+
+        def first_product(b):
+            cat_codes, cat_scales = held["cat_codes", b], held["cat_scales", b]
             h_grp = work.tile([P, BLOCK, PACK], BF16, align_bytes=64)
             for a in range(ROW_TILES):
                 cols = slice(a * P, (a + 1) * P)
@@ -220,14 +232,44 @@ def tile_memorylayercell_pa_t_kernel(
                     in1=b1_col.unsqueeze(1).to_broadcast([P, P, PACK]),
                     op=ALU.add,
                 )
+            held["h_grp", b] = h_grp
+
+        def quantise_h(b):
             h_codes = work.tile([P, BLOCK], U32, align_bytes=64)
             h_scales = work.tile([P, BLOCK], U8, align_bytes=64)
             nc.vector.quantize_mx(
-                out=h_codes[:].bitcast(FP8X4), scales=h_scales[:], in_=h_grp[:].rearrange("m r c -> m (r c)")
+                out=h_codes[:].bitcast(FP8X4), scales=h_scales[:],
+                in_=held["h_grp", b][:].rearrange("m r c -> m (r c)"),
             )
+            held["h_codes", b] = h_codes
+            held["h_scales", b] = h_scales
 
-            v = st_grp[:].rearrange("p (r q) -> p r q", q=PLANES)
-            gate = work.tile([P, 2, PLANES, BLOCK], F32, bufs=3)
+        def second_product(b):
+            for u in range(2):
+                pre_acc = psum.tile([P, BLOCK], F32, tag="mx_acc")
+                nc.tensor.matmul_mx(
+                    out=pre_acc[:],
+                    lhsT=w2_codes[:, u * P : (u + 1) * P].bitcast(FP8X4),
+                    lhsT_scale=w2_scales[:, u * P : (u + 1) * P],
+                    rhs=held["h_codes", b][:].bitcast(FP8X4),
+                    rhs_scale=held["h_scales", b][:],
+                    start=True,
+                    stop=True,
+                )
+                held["pre_acc%d" % u, b] = pre_acc
+
+        def drive_term(b):
+            drive = work.tile([P, PLANES, BLOCK], F32)
+            for q in range(PLANES):
+                nc.scalar.activation(
+                    out=drive[:, q, :], in_=held["pre_acc%d" % (q // 2), b][:], func=ACT.Identity,
+                    scale=drive_scale[:, q : q + 1], bias=drive_bias[:, q : q + 1],
+                )
+            held["drive", b] = drive
+
+        def gates(b):
+            v = held["st_grp", b][:].rearrange("p (r q) -> p r q", q=PLANES)
+            gate = work.tile([P, 2, PLANES, BLOCK], F32)
             for q in range(PLANES):
                 for k in range(2):
                     seen = q if k == 0 else q ^ 1
@@ -240,69 +282,68 @@ def tile_memorylayercell_pa_t_kernel(
                         scalar1=neg_gain[k][:, q : q + 1], scalar2=gate_offset[:, k : k + 1],
                         op0=ALU.mult, op1=ALU.add,
                     )
+            held["gate", b] = gate
 
-            st_words = st_sb[:].bitcast(F32).rearrange("p (a w) -> p a w", a=ROW_TILES)
+        def transpose_states(b):
             for half in range(2):
-                rows = slice(half * 2 * P, (half + 1) * 2 * P)
-                st_v = psum.tile([P, 2, 2 * P], F32)
-                for u in range(2):
-                    for al in range(2):
-                        nc.tensor.transpose(
-                            out=st_v[:, u, al * P : (al + 1) * P],
-                            in_=st_words[:, 2 * half + al, u * P : (u + 1) * P],
-                            identity=ident[:],
-                        )
-                v_psum = st_v[:].bitcast(BF16).rearrange("p u (r e) -> p u r e", e=2)
-                for q in range(PLANES):
-                    for k in range(2):
-                        nc.vector.scalar_tensor_tensor(
-                            out=gate[:, k, q, rows], in0=v_psum[:, q // 2, :, q % 2],
-                            scalar=reversal[k][:, q : q + 1], in1=gate[:, k, q, rows],
-                            op0=ALU.subtract, op1=ALU.mult,
-                        )
-            drive = work.tile([P, PLANES, BLOCK], F32)
-            for u in range(2):
-                pre_acc = psum.tile([P, BLOCK], F32, tag="mx_acc")
-                nc.tensor.matmul_mx(
-                    out=pre_acc[:],
-                    lhsT=w2_codes[:, u * P : (u + 1) * P].bitcast(FP8X4),
-                    lhsT_scale=w2_scales[:, u * P : (u + 1) * P],
-                    rhs=h_codes[:].bitcast(FP8X4),
-                    rhs_scale=h_scales[:],
-                    start=True,
-                    stop=True,
-                )
-                for e in range(2):
-                    q = 2 * u + e
-                    nc.scalar.activation(
-                        out=drive[:, q, :], in_=pre_acc[:], func=ACT.Identity,
-                        scale=drive_scale[:, q : q + 1], bias=drive_bias[:, q : q + 1],
+                st_v = psum.tile([P, 2, HALF], F32)
+                transpose_words(st_v, held["st_sb", b], half)
+                held["st_v%d" % half, b] = st_v
+
+        def currents(b, half):
+            gate = held["gate", b]
+            rows = slice(half * HALF, (half + 1) * HALF)
+            v_psum = held["st_v%d" % half, b][:].bitcast(BF16).rearrange("p u (r e) -> p u r e", e=2)
+            for q in range(PLANES):
+                for k in range(2):
+                    nc.vector.scalar_tensor_tensor(
+                        out=gate[:, k, q, rows], in0=v_psum[:, q // 2, :, q % 2],
+                        scalar=reversal[k][:, q : q + 1], in1=gate[:, k, q, rows],
+                        op0=ALU.subtract, op1=ALU.mult,
                     )
 
-            mean_var = work.tile([P, ROW_TILES, 2], F32)
-            centred = work.tile([P, ROW_TILES, S], F32, bufs=3)
-            for a in range(ROW_TILES):
-                cols = slice(a * P, (a + 1) * P)
-                x_acc = psum.tile([P, S], F32)
-                for q in range(PLANES):
-                    terms = (gate[:, 0, q, cols], gate[:, 1, q, cols], drive[:, q, cols])
-                    for i, term in enumerate(terms):
-                        nc.tensor.matmul(
-                            out=x_acc[:, q * P : (q + 1) * P], lhsT=term, rhs=ident[:], is_transpose=True,
-                            start=(i == 0), stop=(i == len(terms) - 1),
-                        )
-                stats = work.tile([P, 6], F32)
-                nc.vector.bn_stats(out=stats[:], in_=x_acc[:])
-                nc.vector.bn_aggr(out=mean_var[:, a, :], in_=stats[:])
+        def gather_rows(b, a):
+            gate, drive = held["gate", b], held["drive", b]
+            cols = slice(a * P, (a + 1) * P)
+            x_acc = psum.tile([P, S], F32)
+            for q in range(PLANES):
+                terms = (gate[:, 0, q, cols], gate[:, 1, q, cols], drive[:, q, cols])
+                for i, term in enumerate(terms):
+                    nc.tensor.matmul(
+                        out=x_acc[:, q * P : (q + 1) * P], lhsT=term, rhs=ident[:], is_transpose=True,
+                        start=(i == 0), stop=(i == len(terms) - 1),
+                    )
+            held["x_acc%d" % a, b] = x_acc
+
+        def statistics(b, first):
+            if first == 0:
+                mean_var = work.tile([P, ROW_TILES, 2], F32)
+                centred = work.tile([P, ROW_TILES, S], F32)
+                held["mean_var", b] = mean_var
+                held["centred", b] = centred
+            mean_var, centred = held["mean_var", b], held["centred", b]
+            both = (first, first + 1)
+            stats = work.tile([P, 2, 6], F32)
+            for a in both:
+                nc.vector.bn_stats(out=stats[:, a - first, :], in_=held["x_acc%d" % a, b][:])
+            for a in both:
+                nc.vector.bn_aggr(out=mean_var[:, a, :], in_=stats[:, a - first, :])
+            for a in both:
                 nc.vector.scalar_tensor_tensor(
-                    out=centred[:, a, :], in0=x_acc[:], scalar=mean_var[:, a, 0:1], in1=gamma_planes[:],
-                    op0=ALU.subtract, op1=ALU.mult,
+                    out=centred[:, a, :], in0=held["x_acc%d" % a, b][:], scalar=mean_var[:, a, 0:1],
+                    in1=gamma_planes[:], op0=ALU.subtract, op1=ALU.mult,
                 )
+
+        def inverse_std(b):
             var_eps = work.tile([P, ROW_TILES], F32)
-            nc.gpsimd.tensor_scalar_add(out=var_eps[:], in0=mean_var[:, :, 1], scalar1=EPS)
+            nc.gpsimd.tensor_scalar_add(out=var_eps[:], in0=held["mean_var", b][:, :, 1], scalar1=EPS)
             rstd = work.tile([P, ROW_TILES], F32)
             nc.gpsimd.tensor_tensor(out=rstd[:], in0=var_eps[:], in1=neg_half[:], op=ALU.pow)
-            out_sb = work.tile([P, ROW_TILES, S], F32, bufs=3)
+            held["rstd", b] = rstd
+
+        def scale_shift_store(b):
+            centred, rstd = held["centred", b], held["rstd", b]
+            out_sb = work.tile([P, ROW_TILES, S], F32)
             for a in range(ROW_TILES):
                 nc.scalar.activation(
                     out=out_sb[:, a, :].rearrange("r (u j e) -> r u j e", u=2, e=2),
@@ -317,3 +358,28 @@ def tile_memorylayercell_pa_t_kernel(
                 out=out[b * BLOCK : (b + 1) * BLOCK, :].rearrange("(p a) c -> p (a c)", a=ROW_TILES),
                 in_=out_sb[:].rearrange("p a c -> p (a c)"),
             )
+
+        def run(stage, b, *args):
+            if 0 <= b < N_BLOCKS:
+                stage(b, *args)
+
+        for i in range(-2, N_BLOCKS + 1):
+            run(load, i + 3)
+            run(quantise_cat, i + 1)
+            run(drive_term, i)
+            run(inverse_std, i - 1)
+            run(currents, i, 0)
+            run(first_product, i + 1)
+            run(gather_rows, i, 0)
+            run(gather_rows, i, 1)
+            run(gates, i + 1)
+            run(currents, i, 1)
+            run(transpose_cat, i + 2)
+            run(transpose_states, i + 1)
+            run(scale_shift_store, i - 1)
+            run(statistics, i, 0)
+            run(quantise_h, i + 1)
+            run(gather_rows, i, 2)
+            run(gather_rows, i, 3)
+            run(second_product, i + 1)
+            run(statistics, i, 2)

@@ -76,7 +76,7 @@ def tile_memorylayercell_pa_t_kernel(
             rows = slice(b * BLOCK, (b + 1) * BLOCK)
             in_sb = rows_in.tile([P, ROW_TILES * D], BF16)
             nc.sync.dma_start(out=in_sb[:], in_=inputs[rows, :].rearrange("(p a) d -> p (a d)", a=ROW_TILES))
-            st_sb = rows_in.tile([P, ROW_TILES * S], BF16)
+            st_sb = rows_in.tile([P, ROW_TILES * S], BF16, bufs=4)
             nc.sync.dma_start(out=st_sb[:], in_=states[rows, :].rearrange("(p a) d -> p (a d)", a=ROW_TILES))
             held["in_sb", b] = in_sb
             held["st_sb", b] = st_sb
@@ -176,6 +176,10 @@ def tile_memorylayercell_pa_t_kernel(
         beta_f32 = consts.tile([P, S], F32)
         nc.vector.tensor_copy(out=beta_f32[:], in_=beta_rows[:])
 
+        def run(stage, b, *args):
+            if 0 <= b < N_BLOCKS:
+                stage(b, *args)
+
         def transpose_words(dst, src_sb, half):
             words = src_sb[:].bitcast(F32).rearrange("p (a w) -> p a w", a=ROW_TILES)
             for u in range(2):
@@ -186,18 +190,17 @@ def tile_memorylayercell_pa_t_kernel(
                         identity=ident[:],
                     )
 
-        def transpose_cat(b):
-            for name in ("in", "st"):
+        def transpose_cat(b, name, half):
+            if half == 0:
                 grp = work.tile([P, BLOCK * PACK], BF16, align_bytes=64, name=name + "_grp")
                 held[name + "_grp", b] = grp
-                grp_words = grp[:].bitcast(F32).rearrange("p (r u) -> p r u", u=2)
-                for half in range(2):
-                    cat_t = psum.tile([P, 2, HALF], F32)
-                    transpose_words(cat_t, held[name + "_sb", b], half)
-                    nc.scalar.copy(
-                        out=grp_words[:, half * HALF : (half + 1) * HALF, :],
-                        in_=cat_t[:].rearrange("p u r -> p r u"),
-                    )
+            grp_words = held[name + "_grp", b][:].bitcast(F32).rearrange("p (r u) -> p r u", u=2)
+            cat_t = psum.tile([P, 2, HALF], F32)
+            transpose_words(cat_t, held[name + "_sb", b], half)
+            nc.scalar.copy(
+                out=grp_words[:, half * HALF : (half + 1) * HALF, :],
+                in_=cat_t[:].rearrange("p u r -> p r u"),
+            )
 
         def quantise_cat(b):
             cat_codes = work.tile([P, 2, BLOCK], U32, align_bytes=64)
@@ -209,30 +212,30 @@ def tile_memorylayercell_pa_t_kernel(
             held["cat_codes", b] = cat_codes
             held["cat_scales", b] = cat_scales
 
-        def first_product(b):
+        def first_product(b, a):
             cat_codes, cat_scales = held["cat_codes", b], held["cat_scales", b]
-            h_grp = work.tile([P, BLOCK, PACK], BF16, align_bytes=64)
-            for a in range(ROW_TILES):
-                cols = slice(a * P, (a + 1) * P)
-                h_acc = psum.tile([P, PACK, P], F32, tag="mx_acc")
-                for c in range(PACK):
-                    for g in range(2):
-                        nc.tensor.matmul_mx(
-                            out=h_acc[:, c, :],
-                            lhsT=w1_codes[:, g, c * P : (c + 1) * P].bitcast(FP8X4),
-                            lhsT_scale=w1_scales[:, g, c * P : (c + 1) * P],
-                            rhs=cat_codes[:, g, cols].bitcast(FP8X4),
-                            rhs_scale=cat_scales[:, g, cols],
-                            start=(g == 0),
-                            stop=(g == 1),
-                        )
-                nc.vector.tensor_tensor(
-                    out=h_grp[:, cols, :],
-                    in0=h_acc[:].rearrange("m c r -> m r c"),
-                    in1=b1_col.unsqueeze(1).to_broadcast([P, P, PACK]),
-                    op=ALU.add,
-                )
-            held["h_grp", b] = h_grp
+            if a == 0:
+                h_grp = work.tile([P, BLOCK, PACK], BF16, align_bytes=64)
+                held["h_grp", b] = h_grp
+            cols = slice(a * P, (a + 1) * P)
+            h_acc = psum.tile([P, PACK, P], F32, tag="mx_acc")
+            for c in range(PACK):
+                for g in range(2):
+                    nc.tensor.matmul_mx(
+                        out=h_acc[:, c, :],
+                        lhsT=w1_codes[:, g, c * P : (c + 1) * P].bitcast(FP8X4),
+                        lhsT_scale=w1_scales[:, g, c * P : (c + 1) * P],
+                        rhs=cat_codes[:, g, cols].bitcast(FP8X4),
+                        rhs_scale=cat_scales[:, g, cols],
+                        start=(g == 0),
+                        stop=(g == 1),
+                    )
+            nc.vector.tensor_tensor(
+                out=held["h_grp", b][:, cols, :],
+                in0=h_acc[:].rearrange("m c r -> m r c"),
+                in1=b1_col.unsqueeze(1).to_broadcast([P, P, PACK]),
+                op=ALU.add,
+            )
 
         def quantise_h(b):
             h_codes = work.tile([P, BLOCK], U32, align_bytes=64)
@@ -267,10 +270,13 @@ def tile_memorylayercell_pa_t_kernel(
                 )
             held["drive", b] = drive
 
-        def gates(b):
+        def gates(b, u):
             v = held["st_grp", b][:].rearrange("p (r q) -> p r q", q=PLANES)
-            gate = work.tile([P, 2, PLANES, BLOCK], F32)
-            for q in range(PLANES):
+            if u == 0:
+                gate = work.tile([P, 2, PLANES, BLOCK], F32, bufs=3)
+                held["gate", b] = gate
+            gate = held["gate", b]
+            for q in (2 * u, 2 * u + 1):
                 for k in range(2):
                     seen = q if k == 0 else q ^ 1
                     nc.scalar.activation(
@@ -282,25 +288,23 @@ def tile_memorylayercell_pa_t_kernel(
                         scalar1=neg_gain[k][:, q : q + 1], scalar2=gate_offset[:, k : k + 1],
                         op0=ALU.mult, op1=ALU.add,
                     )
-            held["gate", b] = gate
 
-        def transpose_states(b):
-            for half in range(2):
-                st_v = psum.tile([P, 2, HALF], F32)
-                transpose_words(st_v, held["st_sb", b], half)
-                held["st_v%d" % half, b] = st_v
+        def transpose_states(b, half):
+            st_v = psum.tile([P, 2, HALF], F32)
+            transpose_words(st_v, held["st_sb", b], half)
+            held["st_v%d" % half, b] = st_v
 
-        def currents(b, half):
+        def currents(b, first, count):
             gate = held["gate", b]
-            rows = slice(half * HALF, (half + 1) * HALF)
-            v_psum = held["st_v%d" % half, b][:].bitcast(BF16).rearrange("p u (r e) -> p u r e", e=2)
-            for q in range(PLANES):
-                for k in range(2):
-                    nc.vector.scalar_tensor_tensor(
-                        out=gate[:, k, q, rows], in0=v_psum[:, q // 2, :, q % 2],
-                        scalar=reversal[k][:, q : q + 1], in1=gate[:, k, q, rows],
-                        op0=ALU.subtract, op1=ALU.mult,
-                    )
+            for n in range(first, first + count):
+                half, q, k = n // 8, (n % 8) // 2, n % 2
+                rows = slice(half * HALF, (half + 1) * HALF)
+                v_psum = held["st_v%d" % half, b][:].bitcast(BF16).rearrange("p u (r e) -> p u r e", e=2)
+                nc.vector.scalar_tensor_tensor(
+                    out=gate[:, k, q, rows], in0=v_psum[:, q // 2, :, q % 2],
+                    scalar=reversal[k][:, q : q + 1], in1=gate[:, k, q, rows],
+                    op0=ALU.subtract, op1=ALU.mult,
+                )
 
         def gather_rows(b, a):
             gate, drive = held["gate", b], held["drive", b]
@@ -315,24 +319,33 @@ def tile_memorylayercell_pa_t_kernel(
                     )
             held["x_acc%d" % a, b] = x_acc
 
-        def statistics(b, first):
-            if first == 0:
+        def row_stats(b, a):
+            stats = work.tile([P, 6], F32)
+            nc.vector.bn_stats(out=stats[:], in_=held["x_acc%d" % a, b][:])
+            held["stats", b] = stats
+
+        def row_mean(b, a):
+            if a == 0:
                 mean_var = work.tile([P, ROW_TILES, 2], F32)
-                centred = work.tile([P, ROW_TILES, S], F32)
                 held["mean_var", b] = mean_var
+            nc.vector.bn_aggr(out=held["mean_var", b][:, a, :], in_=held["stats", b][:])
+
+        def centre(b, a):
+            if a == 0:
+                centred = work.tile([P, ROW_TILES, S], F32)
                 held["centred", b] = centred
-            mean_var, centred = held["mean_var", b], held["centred", b]
-            both = (first, first + 1)
-            stats = work.tile([P, 2, 6], F32)
-            for a in both:
-                nc.vector.bn_stats(out=stats[:, a - first, :], in_=held["x_acc%d" % a, b][:])
-            for a in both:
-                nc.vector.bn_aggr(out=mean_var[:, a, :], in_=stats[:, a - first, :])
-            for a in both:
-                nc.vector.scalar_tensor_tensor(
-                    out=centred[:, a, :], in0=held["x_acc%d" % a, b][:], scalar=mean_var[:, a, 0:1],
-                    in1=gamma_planes[:], op0=ALU.subtract, op1=ALU.mult,
-                )
+            nc.vector.scalar_tensor_tensor(
+                out=held["centred", b][:, a, :], in0=held["x_acc%d" % a, b][:],
+                scalar=held["mean_var", b][:, a, 0:1], in1=gamma_planes[:],
+                op0=ALU.subtract, op1=ALU.mult,
+            )
+
+        def statistics(i, a):
+            run(row_stats, i, a)
+            run(currents, i + 1, 8 + 2 * a, 1)
+            run(row_mean, i, a)
+            run(currents, i + 1, 9 + 2 * a, 1)
+            run(centre, i, a)
 
         def inverse_std(b):
             var_eps = work.tile([P, ROW_TILES], F32)
@@ -359,27 +372,34 @@ def tile_memorylayercell_pa_t_kernel(
                 in_=out_sb[:].rearrange("p a c -> p (a c)"),
             )
 
-        def run(stage, b, *args):
-            if 0 <= b < N_BLOCKS:
-                stage(b, *args)
-
-        for i in range(-2, N_BLOCKS + 1):
-            run(load, i + 3)
-            run(quantise_cat, i + 1)
+        for i in range(-3, N_BLOCKS + 1):
+            run(load, i + 4)
+            run(transpose_states, i + 1, 1)
+            run(quantise_cat, i + 2)
             run(drive_term, i)
             run(inverse_std, i - 1)
-            run(currents, i, 0)
-            run(first_product, i + 1)
+            run(currents, i + 1, 0, 4)
+            run(transpose_cat, i + 3, "in", 0)
+            run(first_product, i + 1, 0)
+            run(currents, i + 1, 4, 2)
+            run(transpose_cat, i + 3, "in", 1)
+            run(first_product, i + 1, 1)
+            run(currents, i + 1, 6, 2)
+            run(gates, i + 2, 0)
             run(gather_rows, i, 0)
+            run(transpose_cat, i + 3, "st", 0)
+            statistics(i, 0)
+            run(first_product, i + 1, 2)
+            run(gates, i + 2, 1)
             run(gather_rows, i, 1)
-            run(gates, i + 1)
-            run(currents, i, 1)
-            run(transpose_cat, i + 2)
-            run(transpose_states, i + 1)
-            run(scale_shift_store, i - 1)
-            run(statistics, i, 0)
-            run(quantise_h, i + 1)
+            run(transpose_cat, i + 3, "st", 1)
+            statistics(i, 1)
+            run(first_product, i + 1, 3)
             run(gather_rows, i, 2)
+            run(transpose_states, i + 2, 0)
+            run(scale_shift_store, i - 1)
+            statistics(i, 2)
+            run(quantise_h, i + 1)
             run(gather_rows, i, 3)
             run(second_product, i + 1)
-            run(statistics, i, 2)
+            statistics(i, 3)

@@ -380,26 +380,26 @@ def tile_memorylayercell_pa_t_kernel(
             run(inverse_std, i - 1)
             run(currents, i + 1, 0, 4)
             run(transpose_cat, i + 3, "in", 0)
+            run(transpose_cat, i + 3, "in", 1)
             run(first_product, i + 1, 0)
             run(currents, i + 1, 4, 2)
-            run(transpose_cat, i + 3, "in", 1)
             run(first_product, i + 1, 1)
             run(currents, i + 1, 6, 2)
             run(gates, i + 2, 0)
             run(gather_rows, i, 0)
             run(transpose_cat, i + 3, "st", 0)
-            statistics(i, 0)
-            run(first_product, i + 1, 2)
-            run(gates, i + 2, 1)
             run(gather_rows, i, 1)
             run(transpose_cat, i + 3, "st", 1)
+            statistics(i, 0)
+            run(gates, i + 2, 1)
             statistics(i, 1)
+            run(first_product, i + 1, 2)
             run(first_product, i + 1, 3)
             run(gather_rows, i, 2)
             run(transpose_states, i + 2, 0)
+            run(gather_rows, i, 3)
             run(scale_shift_store, i - 1)
             statistics(i, 2)
             run(quantise_h, i + 1)
-            run(gather_rows, i, 3)
             run(second_product, i + 1)
             statistics(i, 3)

@@ -310,12 +310,12 @@ def tile_memorylayercell_pa_t_kernel(
             gate, drive = held["gate", b], held["drive", b]
             cols = slice(a * P, (a + 1) * P)
             x_acc = psum.tile([P, S], F32)
-            for q in range(PLANES):
-                terms = (gate[:, 0, q, cols], gate[:, 1, q, cols], drive[:, q, cols])
-                for i, term in enumerate(terms):
+            terms = (gate[:, 0, :, cols], gate[:, 1, :, cols], drive[:, :, cols])
+            for i, term in enumerate(terms):
+                for q in range(PLANES):
                     nc.tensor.matmul(
-                        out=x_acc[:, q * P : (q + 1) * P], lhsT=term, rhs=ident[:], is_transpose=True,
-                        start=(i == 0), stop=(i == len(terms) - 1),
+                        out=x_acc[:, q * P : (q + 1) * P], lhsT=term[:, q, :], rhs=ident[:], is_transpose=True,
+                        start=(i == 0 and q == 0), stop=(i == len(terms) - 1 and q == PLANES - 1),
                     )
             held["x_acc%d" % a, b] = x_acc
 

@@ -21,6 +21,7 @@ BLOCK = ROW_TILES * P
 HALF = BLOCK // 2
 N_BLOCKS = B // BLOCK
 PLANES = 4
+GPSIMD_GATES = ((0, 0), (0, 1), (1, 0))
 
 FLOPS = 2 * B * ((D + S) * S + S * PAIRS)
 
@@ -276,18 +277,35 @@ def tile_memorylayercell_pa_t_kernel(
                 gate = work.tile([P, 2, PLANES, BLOCK], F32, bufs=3)
                 held["gate", b] = gate
             gate = held["gate", b]
-            for q in (2 * u, 2 * u + 1):
-                for k in range(2):
-                    seen = q if k == 0 else q ^ 1
-                    nc.scalar.activation(
-                        out=gate[:, k, q, :], in_=v[:, :, seen], func=ACT.Sigmoid,
-                        scale=slope[k][:, q : q + 1], bias=shift[k][:, q : q + 1],
-                    )
+            def scale_and_offset(engine_is_gpsimd, k, q):
+                if engine_is_gpsimd:
                     nc.gpsimd.tensor_scalar(
                         out=gate[:, k, q, :], in0=gate[:, k, q, :],
                         scalar1=neg_gain[k][:, q : q + 1], scalar2=gate_offset[:, k : k + 1],
                         op0=ALU.mult, op1=ALU.add,
                     )
+                else:
+                    nc.scalar.activation(
+                        out=gate[:, k, q, :], in_=gate[:, k, q, :], func=ACT.Identity,
+                        scale=neg_gain[k][:, q : q + 1], bias=gate_offset[:, k : k + 1],
+                    )
+
+            owed = None
+            for k, q in ((1, 2 * u), (0, 2 * u), (1, 2 * u + 1), (0, 2 * u + 1)):
+                seen = q if k == 0 else q ^ 1
+                nc.scalar.activation(
+                    out=gate[:, k, q, :], in_=v[:, :, seen], func=ACT.Sigmoid,
+                    scale=slope[k][:, q : q + 1], bias=shift[k][:, q : q + 1],
+                )
+                if owed is not None:
+                    scale_and_offset(False, owed[0], owed[1])
+                owed = None
+                if (k, q) in GPSIMD_GATES:
+                    scale_and_offset(True, k, q)
+                else:
+                    owed = (k, q)
+            if owed is not None:
+                scale_and_offset(False, owed[0], owed[1])
 
         def transpose_states(b, half):
             st_v = psum.tile([P, 2, HALF], F32)
@@ -358,10 +376,10 @@ def tile_memorylayercell_pa_t_kernel(
             centred, rstd = held["centred", b], held["rstd", b]
             out_sb = work.tile([P, ROW_TILES, S], F32)
             for a in range(ROW_TILES):
-                nc.scalar.activation(
+                nc.gpsimd.tensor_scalar(
                     out=out_sb[:, a, :].rearrange("r (u j e) -> r u j e", u=2, e=2),
-                    in_=centred[:, a, :].rearrange("r (u e j) -> r u j e", u=2, e=2),
-                    func=ACT.Identity, scale=rstd[:, a : a + 1],
+                    in0=centred[:, a, :].rearrange("r (u e j) -> r u j e", u=2, e=2),
+                    scalar1=rstd[:, a : a + 1], scalar2=0.0, op0=ALU.mult, op1=ALU.add,
                 )
             nc.gpsimd.tensor_tensor(
                 out=out_sb[:], in0=out_sb[:], in1=beta_f32[:].unsqueeze(1).to_broadcast([P, ROW_TILES, S]),
@@ -374,17 +392,15 @@ def tile_memorylayercell_pa_t_kernel(
 
         for i in range(-3, N_BLOCKS + 1):
             run(load, i + 4)
-            run(transpose_states, i + 1, 1)
-            run(quantise_cat, i + 2)
             run(drive_term, i)
             run(inverse_std, i - 1)
-            run(currents, i + 1, 0, 4)
+            run(scale_shift_store, i - 1)
+            run(currents, i + 1, 0, 8)
             run(transpose_cat, i + 3, "in", 0)
             run(transpose_cat, i + 3, "in", 1)
+            run(transpose_states, i + 1, 1)
             run(first_product, i + 1, 0)
-            run(currents, i + 1, 4, 2)
             run(first_product, i + 1, 1)
-            run(currents, i + 1, 6, 2)
             run(gates, i + 2, 0)
             run(gather_rows, i, 0)
             run(transpose_cat, i + 3, "st", 0)
@@ -398,8 +414,11 @@ def tile_memorylayercell_pa_t_kernel(
             run(gather_rows, i, 2)
             run(transpose_states, i + 2, 0)
             run(gather_rows, i, 3)
-            run(scale_shift_store, i - 1)
             statistics(i, 2)
             run(quantise_h, i + 1)
             run(second_product, i + 1)
-            statistics(i, 3)
+            run(row_stats, i, 3)
+            run(quantise_cat, i + 3)
+            run(row_mean, i, 3)
+            run(currents, i + 1, 14, 2)
+            run(centre, i, 3)

@@ -20,8 +20,10 @@ ROW_TILES = 4
 BLOCK = ROW_TILES * P
 HALF = BLOCK // 2
 N_BLOCKS = B // BLOCK
+LAST = N_BLOCKS - 1
 PLANES = 4
-GPSIMD_GATES = ((0, 0), (0, 1), (1, 0))
+GPSIMD_GATES = ((0, 0),)
+TENSOR_GATES = ((1, 0), (1, 1), (1, 2))
 
 FLOPS = 2 * B * ((D + S) * S + S * PAIRS)
 
@@ -154,6 +156,9 @@ def tile_memorylayercell_pa_t_kernel(
             slope.append(slope_k)
             shift.append(shift_k)
             neg_gain.append(neg_gain_k)
+        gain_diag = consts.tile([P, PLANES, P], F32)
+        for q in range(PLANES):
+            nc.vector.tensor_scalar_mul(out=gain_diag[:, q, :], in0=ident[:], scalar1=neg_gain[1][:, q : q + 1])
         gate_offset = consts.tile([P, 2], F32)
         nc.vector.memset(gate_offset[:, 0:1], 1.0)
         nc.vector.memset(gate_offset[:, 1:2], 0.0)
@@ -191,13 +196,13 @@ def tile_memorylayercell_pa_t_kernel(
                         identity=ident[:],
                     )
 
-        def transpose_cat(b, name, half):
-            if half == 0:
-                grp = work.tile([P, BLOCK * PACK], BF16, align_bytes=64, name=name + "_grp")
-                held[name + "_grp", b] = grp
-            grp_words = held[name + "_grp", b][:].bitcast(F32).rearrange("p (r u) -> p r u", u=2)
+        def transpose_cat(b, g, half):
+            if g == 0 and half == 0:
+                cat_grp = work.tile([P, 2, BLOCK * PACK], BF16, align_bytes=64)
+                held["cat_grp", b] = cat_grp
+            grp_words = held["cat_grp", b][:, g, :].bitcast(F32).rearrange("p (r u) -> p r u", u=2)
             cat_t = psum.tile([P, 2, HALF], F32)
-            transpose_words(cat_t, held[name + "_sb", b], half)
+            transpose_words(cat_t, held[("in_sb", "st_sb")[g], b], half)
             nc.scalar.copy(
                 out=grp_words[:, half * HALF : (half + 1) * HALF, :],
                 in_=cat_t[:].rearrange("p u r -> p r u"),
@@ -206,20 +211,19 @@ def tile_memorylayercell_pa_t_kernel(
         def quantise_cat(b):
             cat_codes = work.tile([P, 2, BLOCK], U32, align_bytes=64)
             cat_scales = work.tile([P, 2, BLOCK], U8, align_bytes=64)
-            for g, name in enumerate(("in_grp", "st_grp")):
-                nc.vector.quantize_mx(
-                    out=cat_codes[:, g, :].bitcast(FP8X4), scales=cat_scales[:, g, :], in_=held[name, b][:]
-                )
+            nc.vector.quantize_mx(
+                out=cat_codes[:].rearrange("p g r -> p (g r)").bitcast(FP8X4),
+                scales=cat_scales[:].rearrange("p g r -> p (g r)"),
+                in_=held["cat_grp", b][:].rearrange("p g c -> p (g c)"),
+            )
             held["cat_codes", b] = cat_codes
             held["cat_scales", b] = cat_scales
 
         def first_product(b, a):
             cat_codes, cat_scales = held["cat_codes", b], held["cat_scales", b]
-            if a == 0:
-                h_grp = work.tile([P, BLOCK, PACK], BF16, align_bytes=64)
-                held["h_grp", b] = h_grp
             cols = slice(a * P, (a + 1) * P)
             h_acc = psum.tile([P, PACK, P], F32, tag="mx_acc")
+            held["h_acc%d" % a, b] = h_acc
             for c in range(PACK):
                 for g in range(2):
                     nc.tensor.matmul_mx(
@@ -231,9 +235,14 @@ def tile_memorylayercell_pa_t_kernel(
                         start=(g == 0),
                         stop=(g == 1),
                     )
+
+        def add_bias(b, a):
+            if a == 0:
+                h_grp = work.tile([P, BLOCK, PACK], BF16, align_bytes=64)
+                held["h_grp", b] = h_grp
             nc.vector.tensor_tensor(
-                out=held["h_grp", b][:, cols, :],
-                in0=h_acc[:].rearrange("m c r -> m r c"),
+                out=held["h_grp", b][:, a * P : (a + 1) * P, :],
+                in0=held["h_acc%d" % a, b][:].rearrange("m c r -> m r c"),
                 in1=b1_col.unsqueeze(1).to_broadcast([P, P, PACK]),
                 op=ALU.add,
             )
@@ -272,7 +281,7 @@ def tile_memorylayercell_pa_t_kernel(
             held["drive", b] = drive
 
         def gates(b, u):
-            v = held["st_grp", b][:].rearrange("p (r q) -> p r q", q=PLANES)
+            v = held["cat_grp", b][:, 1, :].rearrange("p (r q) -> p r q", q=PLANES)
             if u == 0:
                 gate = work.tile([P, 2, PLANES, BLOCK], F32, bufs=3)
                 held["gate", b] = gate
@@ -302,27 +311,29 @@ def tile_memorylayercell_pa_t_kernel(
                 owed = None
                 if (k, q) in GPSIMD_GATES:
                     scale_and_offset(True, k, q)
-                else:
+                elif (k, q) not in TENSOR_GATES:
                     owed = (k, q)
             if owed is not None:
                 scale_and_offset(False, owed[0], owed[1])
 
-        def transpose_states(b, half):
-            st_v = psum.tile([P, 2, HALF], F32)
-            transpose_words(st_v, held["st_sb", b], half)
-            held["st_v%d" % half, b] = st_v
-
-        def currents(b, first, count):
-            gate = held["gate", b]
-            for n in range(first, first + count):
-                half, q, k = n // 8, (n % 8) // 2, n % 2
-                rows = slice(half * HALF, (half + 1) * HALF)
-                v_psum = held["st_v%d" % half, b][:].bitcast(BF16).rearrange("p u (r e) -> p u r e", e=2)
-                nc.vector.scalar_tensor_tensor(
-                    out=gate[:, k, q, rows], in0=v_psum[:, q // 2, :, q % 2],
-                    scalar=reversal[k][:, q : q + 1], in1=gate[:, k, q, rows],
-                    op0=ALU.subtract, op1=ALU.mult,
+        def transpose_states(b, u):
+            st_v = psum.tile([P, BLOCK], F32)
+            words = held["st_sb", b][:].bitcast(F32).rearrange("p (a w) -> p a w", a=ROW_TILES)
+            for a in range(ROW_TILES):
+                nc.tensor.transpose(
+                    out=st_v[:, a * P : (a + 1) * P], in_=words[:, a, u * P : (u + 1) * P], identity=ident[:]
                 )
+            held["st_v%d" % u, b] = st_v
+
+        def currents(b, n):
+            q, k = n // 2, n % 2
+            gate = held["gate", b]
+            v_psum = held["st_v%d" % (q // 2), b][:].bitcast(BF16).rearrange("p (r e) -> p r e", e=2)
+            nc.vector.scalar_tensor_tensor(
+                out=gate[:, k, q, :], in0=v_psum[:, :, q % 2],
+                scalar=reversal[k][:, q : q + 1], in1=gate[:, k, q, :],
+                op0=ALU.subtract, op1=ALU.mult,
+            )
 
         def gather_rows(b, a):
             gate, drive = held["gate", b], held["drive", b]
@@ -331,8 +342,10 @@ def tile_memorylayercell_pa_t_kernel(
             terms = (gate[:, 0, :, cols], gate[:, 1, :, cols], drive[:, :, cols])
             for i, term in enumerate(terms):
                 for q in range(PLANES):
+                    scaled = (i, q) in TENSOR_GATES
                     nc.tensor.matmul(
-                        out=x_acc[:, q * P : (q + 1) * P], lhsT=term[:, q, :], rhs=ident[:], is_transpose=True,
+                        out=x_acc[:, q * P : (q + 1) * P], lhsT=term[:, q, :],
+                        rhs=gain_diag[:, q, :] if scaled else ident[:], is_transpose=not scaled,
                         start=(i == 0 and q == 0), stop=(i == len(terms) - 1 and q == PLANES - 1),
                     )
             held["x_acc%d" % a, b] = x_acc
@@ -358,12 +371,18 @@ def tile_memorylayercell_pa_t_kernel(
                 op0=ALU.subtract, op1=ALU.mult,
             )
 
-        def statistics(i, a):
+        def statistics(i, a, filler1, filler2):
             run(row_stats, i, a)
-            run(currents, i + 1, 8 + 2 * a, 1)
+            if i == LAST:
+                last_shift_store(i - 1, a)
+            filler1()
             run(row_mean, i, a)
-            run(currents, i + 1, 9 + 2 * a, 1)
+            filler2()
             run(centre, i, a)
+            if i == LAST:
+                last_scale(i, a)
+                if a > 0:
+                    last_shift_store(i, a - 1)
 
         def inverse_std(b):
             var_eps = work.tile([P, ROW_TILES], F32)
@@ -390,35 +409,67 @@ def tile_memorylayercell_pa_t_kernel(
                 in_=out_sb[:].rearrange("p a c -> p (a c)"),
             )
 
-        for i in range(-3, N_BLOCKS + 1):
+        def last_scale(b, a):
+            if a == 0:
+                var_eps = work.tile([P, ROW_TILES], F32)
+                rstd = work.tile([P, ROW_TILES], F32)
+                out_sb = work.tile([P, ROW_TILES, S], F32)
+                held["var_eps", b], held["rstd", b], held["out_sb", b] = var_eps, rstd, out_sb
+            var_eps, rstd = held["var_eps", b], held["rstd", b]
+            nc.gpsimd.tensor_scalar_add(
+                out=var_eps[:, a : a + 1], in0=held["mean_var", b][:, a, 1:2], scalar1=EPS
+            )
+            nc.gpsimd.tensor_tensor(
+                out=rstd[:, a : a + 1], in0=var_eps[:, a : a + 1], in1=neg_half[:, a : a + 1], op=ALU.pow
+            )
+            nc.scalar.activation(
+                out=held["out_sb", b][:, a, :].rearrange("r (u j e) -> r u j e", u=2, e=2),
+                in_=held["centred", b][:, a, :].rearrange("r (u e j) -> r u j e", u=2, e=2),
+                func=ACT.Identity, scale=rstd[:, a : a + 1],
+            )
+
+        def last_shift_store(b, a):
+            out_sb = held["out_sb", b]
+            nc.vector.tensor_tensor(out=out_sb[:, a, :], in0=out_sb[:, a, :], in1=beta_f32[:], op=ALU.add)
+            nc.sync.dma_start(
+                out=out[b * BLOCK : (b + 1) * BLOCK, :].rearrange("(p a) c -> p a c", a=ROW_TILES)[:, a, :],
+                in_=out_sb[:, a, :],
+            )
+
+        for i in range(-3, N_BLOCKS):
             run(load, i + 4)
             run(drive_term, i)
-            run(inverse_std, i - 1)
-            run(scale_shift_store, i - 1)
-            run(currents, i + 1, 0, 8)
-            run(transpose_cat, i + 3, "in", 0)
-            run(transpose_cat, i + 3, "in", 1)
+            if i == LAST:
+                for a in range(ROW_TILES):
+                    last_scale(i - 1, a)
+            else:
+                run(inverse_std, i - 1)
+                run(scale_shift_store, i - 1)
+            run(currents, i + 1, 1)
+            run(currents, i + 1, 2)
+            run(transpose_cat, i + 3, 0, 0)
+            run(transpose_cat, i + 3, 0, 1)
             run(transpose_states, i + 1, 1)
             run(first_product, i + 1, 0)
             run(first_product, i + 1, 1)
+            run(add_bias, i + 1, 0)
+            run(currents, i + 1, 3)
+            run(add_bias, i + 1, 1)
+            run(currents, i + 1, 7)
             run(gates, i + 2, 0)
             run(gather_rows, i, 0)
-            run(transpose_cat, i + 3, "st", 0)
+            run(transpose_cat, i + 3, 1, 0)
             run(gather_rows, i, 1)
-            run(transpose_cat, i + 3, "st", 1)
-            statistics(i, 0)
+            run(transpose_cat, i + 3, 1, 1)
+            statistics(i, 0, lambda: run(currents, i + 1, 4), lambda: run(currents, i + 1, 5))
             run(gates, i + 2, 1)
-            statistics(i, 1)
             run(first_product, i + 1, 2)
             run(first_product, i + 1, 3)
+            statistics(i, 1, lambda: run(add_bias, i + 1, 2), lambda: run(add_bias, i + 1, 3))
             run(gather_rows, i, 2)
             run(transpose_states, i + 2, 0)
             run(gather_rows, i, 3)
-            statistics(i, 2)
-            run(quantise_h, i + 1)
+            statistics(i, 2, lambda: run(quantise_h, i + 1), lambda: run(currents, i + 1, 6))
             run(second_product, i + 1)
-            run(row_stats, i, 3)
-            run(quantise_cat, i + 3)
-            run(row_mean, i, 3)
-            run(currents, i + 1, 14, 2)
-            run(centre, i, 3)
+            statistics(i, 3, lambda: run(quantise_cat, i + 3), lambda: run(currents, i + 2, 0))
+        last_shift_store(LAST, 3)

@@ -17,13 +17,13 @@ B, D, S = 8192, 512, 512
 PAIRS = S // 2
 EPS = 1e-6
 ROW_TILES = 4
-BLOCK = ROW_TILES * P
-HALF = BLOCK // 2
-N_BLOCKS = B // BLOCK
-LAST = N_BLOCKS - 1
+CHUNK = ROW_TILES * P
+HALF = CHUNK // 2
+N_CHUNKS = B // CHUNK
+LAST = N_CHUNKS - 1
 PLANES = 4
+TENSOR_PLANES = (0, 1, 2)
 GPSIMD_GATES = ((0, 0),)
-TENSOR_GATES = ((1, 0), (1, 1), (1, 2))
 
 FLOPS = 2 * B * ((D + S) * S + S * PAIRS)
 
@@ -75,14 +75,14 @@ def tile_memorylayercell_pa_t_kernel(
         stack.enter_context(tc.manual_schedule())
         held = {}
 
-        def load(b):
-            rows = slice(b * BLOCK, (b + 1) * BLOCK)
+        def load(ch):
+            rows = slice(ch * CHUNK, (ch + 1) * CHUNK)
             in_sb = rows_in.tile([P, ROW_TILES * D], BF16)
             nc.sync.dma_start(out=in_sb[:], in_=inputs[rows, :].rearrange("(p a) d -> p (a d)", a=ROW_TILES))
             st_sb = rows_in.tile([P, ROW_TILES * S], BF16, bufs=4)
             nc.sync.dma_start(out=st_sb[:], in_=states[rows, :].rearrange("(p a) d -> p (a d)", a=ROW_TILES))
-            held["in_sb", b] = in_sb
-            held["st_sb", b] = st_sb
+            held["in_sb", ch] = in_sb
+            held["st_sb", ch] = st_sb
 
         w1_raw = consts.tile([P, 2, PACK, S], BF16)
         nc.sync.dma_start(
@@ -157,7 +157,7 @@ def tile_memorylayercell_pa_t_kernel(
             shift.append(shift_k)
             neg_gain.append(neg_gain_k)
         gain_diag = consts.tile([P, PLANES, P], F32)
-        for q in range(PLANES):
+        for q in TENSOR_PLANES:
             nc.vector.tensor_scalar_mul(out=gain_diag[:, q, :], in0=ident[:], scalar1=neg_gain[1][:, q : q + 1])
         gate_offset = consts.tile([P, 2], F32)
         nc.vector.memset(gate_offset[:, 0:1], 1.0)
@@ -182,48 +182,45 @@ def tile_memorylayercell_pa_t_kernel(
         beta_f32 = consts.tile([P, S], F32)
         nc.vector.tensor_copy(out=beta_f32[:], in_=beta_rows[:])
 
-        def run(stage, b, *args):
-            if 0 <= b < N_BLOCKS:
-                stage(b, *args)
+        def run(stage, ch, *args):
+            if 0 <= ch < N_CHUNKS:
+                stage(ch, *args)
 
-        def transpose_words(dst, src_sb, half):
-            words = src_sb[:].bitcast(F32).rearrange("p (a w) -> p a w", a=ROW_TILES)
+        def transpose_cat(ch, g, half):
+            if g == 0 and half == 0:
+                cat_grp = work.tile([P, 2, CHUNK * PACK], BF16, align_bytes=64)
+                held["cat_grp", ch] = cat_grp
+            grp_words = held["cat_grp", ch][:, g, :].bitcast(F32).rearrange("p (r u) -> p r u", u=2)
+            words = held[("in_sb", "st_sb")[g], ch][:].bitcast(F32).rearrange("p (a w) -> p a w", a=ROW_TILES)
+            cat_t = psum.tile([P, 2, HALF], F32)
             for u in range(2):
                 for al in range(2):
                     nc.tensor.transpose(
-                        out=dst[:, u, al * P : (al + 1) * P],
+                        out=cat_t[:, u, al * P : (al + 1) * P],
                         in_=words[:, 2 * half + al, u * P : (u + 1) * P],
                         identity=ident[:],
                     )
-
-        def transpose_cat(b, g, half):
-            if g == 0 and half == 0:
-                cat_grp = work.tile([P, 2, BLOCK * PACK], BF16, align_bytes=64)
-                held["cat_grp", b] = cat_grp
-            grp_words = held["cat_grp", b][:, g, :].bitcast(F32).rearrange("p (r u) -> p r u", u=2)
-            cat_t = psum.tile([P, 2, HALF], F32)
-            transpose_words(cat_t, held[("in_sb", "st_sb")[g], b], half)
             nc.scalar.copy(
                 out=grp_words[:, half * HALF : (half + 1) * HALF, :],
                 in_=cat_t[:].rearrange("p u r -> p r u"),
             )
 
-        def quantise_cat(b):
-            cat_codes = work.tile([P, 2, BLOCK], U32, align_bytes=64)
-            cat_scales = work.tile([P, 2, BLOCK], U8, align_bytes=64)
+        def quantise_cat(ch):
+            cat_codes = work.tile([P, 2, CHUNK], U32, align_bytes=64)
+            cat_scales = work.tile([P, 2, CHUNK], U8, align_bytes=64)
             nc.vector.quantize_mx(
                 out=cat_codes[:].rearrange("p g r -> p (g r)").bitcast(FP8X4),
                 scales=cat_scales[:].rearrange("p g r -> p (g r)"),
-                in_=held["cat_grp", b][:].rearrange("p g c -> p (g c)"),
+                in_=held["cat_grp", ch][:].rearrange("p g c -> p (g c)"),
             )
-            held["cat_codes", b] = cat_codes
-            held["cat_scales", b] = cat_scales
+            held["cat_codes", ch] = cat_codes
+            held["cat_scales", ch] = cat_scales
 
-        def first_product(b, a):
-            cat_codes, cat_scales = held["cat_codes", b], held["cat_scales", b]
+        def first_product(ch, a):
+            cat_codes, cat_scales = held["cat_codes", ch], held["cat_scales", ch]
             cols = slice(a * P, (a + 1) * P)
             h_acc = psum.tile([P, PACK, P], F32, tag="mx_acc")
-            held["h_acc%d" % a, b] = h_acc
+            held["h_acc%d" % a, ch] = h_acc
             for c in range(PACK):
                 for g in range(2):
                     nc.tensor.matmul_mx(
@@ -236,68 +233,62 @@ def tile_memorylayercell_pa_t_kernel(
                         stop=(g == 1),
                     )
 
-        def add_bias(b, a):
+        def add_bias(ch, a):
             if a == 0:
-                h_grp = work.tile([P, BLOCK, PACK], BF16, align_bytes=64)
-                held["h_grp", b] = h_grp
+                h_grp = work.tile([P, CHUNK, PACK], BF16, align_bytes=64)
+                held["h_grp", ch] = h_grp
             nc.vector.tensor_tensor(
-                out=held["h_grp", b][:, a * P : (a + 1) * P, :],
-                in0=held["h_acc%d" % a, b][:].rearrange("m c r -> m r c"),
+                out=held["h_grp", ch][:, a * P : (a + 1) * P, :],
+                in0=held["h_acc%d" % a, ch][:].rearrange("m c r -> m r c"),
                 in1=b1_col.unsqueeze(1).to_broadcast([P, P, PACK]),
                 op=ALU.add,
             )
 
-        def quantise_h(b):
-            h_codes = work.tile([P, BLOCK], U32, align_bytes=64)
-            h_scales = work.tile([P, BLOCK], U8, align_bytes=64)
+        def quantise_h(ch):
+            h_codes = work.tile([P, CHUNK], U32, align_bytes=64)
+            h_scales = work.tile([P, CHUNK], U8, align_bytes=64)
             nc.vector.quantize_mx(
                 out=h_codes[:].bitcast(FP8X4), scales=h_scales[:],
-                in_=held["h_grp", b][:].rearrange("m r c -> m (r c)"),
+                in_=held["h_grp", ch][:].rearrange("m r c -> m (r c)"),
             )
-            held["h_codes", b] = h_codes
-            held["h_scales", b] = h_scales
+            held["h_codes", ch] = h_codes
+            held["h_scales", ch] = h_scales
 
-        def second_product(b):
+        def second_product(ch):
             for u in range(2):
-                pre_acc = psum.tile([P, BLOCK], F32, tag="mx_acc")
+                pre_acc = psum.tile([P, CHUNK], F32, tag="mx_acc")
                 nc.tensor.matmul_mx(
                     out=pre_acc[:],
                     lhsT=w2_codes[:, u * P : (u + 1) * P].bitcast(FP8X4),
                     lhsT_scale=w2_scales[:, u * P : (u + 1) * P],
-                    rhs=held["h_codes", b][:].bitcast(FP8X4),
-                    rhs_scale=held["h_scales", b][:],
+                    rhs=held["h_codes", ch][:].bitcast(FP8X4),
+                    rhs_scale=held["h_scales", ch][:],
                     start=True,
                     stop=True,
                 )
-                held["pre_acc%d" % u, b] = pre_acc
+                held["pre_acc%d" % u, ch] = pre_acc
 
-        def drive_term(b):
-            drive = work.tile([P, PLANES, BLOCK], F32)
+        def drive_term(ch):
+            drive = work.tile([P, PLANES, CHUNK], F32)
             for q in range(PLANES):
                 nc.scalar.activation(
-                    out=drive[:, q, :], in_=held["pre_acc%d" % (q // 2), b][:], func=ACT.Identity,
+                    out=drive[:, q, :], in_=held["pre_acc%d" % (q // 2), ch][:], func=ACT.Identity,
                     scale=drive_scale[:, q : q + 1], bias=drive_bias[:, q : q + 1],
                 )
-            held["drive", b] = drive
+            held["drive", ch] = drive
 
-        def gates(b, u):
-            v = held["cat_grp", b][:, 1, :].rearrange("p (r q) -> p r q", q=PLANES)
+        def gates(ch, u):
+            v = held["cat_grp", ch][:, 1, :].rearrange("p (r q) -> p r q", q=PLANES)
             if u == 0:
-                gate = work.tile([P, 2, PLANES, BLOCK], F32, bufs=3)
-                held["gate", b] = gate
-            gate = held["gate", b]
-            def scale_and_offset(engine_is_gpsimd, k, q):
-                if engine_is_gpsimd:
-                    nc.gpsimd.tensor_scalar(
-                        out=gate[:, k, q, :], in0=gate[:, k, q, :],
-                        scalar1=neg_gain[k][:, q : q + 1], scalar2=gate_offset[:, k : k + 1],
-                        op0=ALU.mult, op1=ALU.add,
-                    )
-                else:
-                    nc.scalar.activation(
-                        out=gate[:, k, q, :], in_=gate[:, k, q, :], func=ACT.Identity,
-                        scale=neg_gain[k][:, q : q + 1], bias=gate_offset[:, k : k + 1],
-                    )
+                gate = work.tile([P, 2, PLANES, CHUNK], F32, bufs=3)
+                held["gate", ch] = gate
+            gate = held["gate", ch]
+
+            def scale_on_scalar(k, q):
+                nc.scalar.activation(
+                    out=gate[:, k, q, :], in_=gate[:, k, q, :], func=ACT.Identity,
+                    scale=neg_gain[k][:, q : q + 1], bias=gate_offset[:, k : k + 1],
+                )
 
             owed = None
             for k, q in ((1, 2 * u), (0, 2 * u), (1, 2 * u + 1), (0, 2 * u + 1)):
@@ -307,97 +298,88 @@ def tile_memorylayercell_pa_t_kernel(
                     scale=slope[k][:, q : q + 1], bias=shift[k][:, q : q + 1],
                 )
                 if owed is not None:
-                    scale_and_offset(False, owed[0], owed[1])
+                    scale_on_scalar(owed[0], owed[1])
                 owed = None
                 if (k, q) in GPSIMD_GATES:
-                    scale_and_offset(True, k, q)
-                elif (k, q) not in TENSOR_GATES:
+                    nc.gpsimd.tensor_scalar(
+                        out=gate[:, k, q, :], in0=gate[:, k, q, :],
+                        scalar1=neg_gain[k][:, q : q + 1], scalar2=gate_offset[:, k : k + 1],
+                        op0=ALU.mult, op1=ALU.add,
+                    )
+                elif k == 0 or q not in TENSOR_PLANES:
                     owed = (k, q)
             if owed is not None:
-                scale_and_offset(False, owed[0], owed[1])
+                scale_on_scalar(owed[0], owed[1])
 
-        def transpose_states(b, u):
-            st_v = psum.tile([P, BLOCK], F32)
-            words = held["st_sb", b][:].bitcast(F32).rearrange("p (a w) -> p a w", a=ROW_TILES)
+        def transpose_states(ch, u):
+            st_v = psum.tile([P, CHUNK], F32)
+            words = held["st_sb", ch][:].bitcast(F32).rearrange("p (a w) -> p a w", a=ROW_TILES)
             for a in range(ROW_TILES):
                 nc.tensor.transpose(
                     out=st_v[:, a * P : (a + 1) * P], in_=words[:, a, u * P : (u + 1) * P], identity=ident[:]
                 )
-            held["st_v%d" % u, b] = st_v
+            held["st_v%d" % u, ch] = st_v
 
-        def currents(b, n):
-            q, k = n // 2, n % 2
-            gate = held["gate", b]
-            v_psum = held["st_v%d" % (q // 2), b][:].bitcast(BF16).rearrange("p (r e) -> p r e", e=2)
+        def current(ch, q, k):
+            gate = held["gate", ch]
+            v_psum = held["st_v%d" % (q // 2), ch][:].bitcast(BF16).rearrange("p (r e) -> p r e", e=2)
             nc.vector.scalar_tensor_tensor(
                 out=gate[:, k, q, :], in0=v_psum[:, :, q % 2],
                 scalar=reversal[k][:, q : q + 1], in1=gate[:, k, q, :],
                 op0=ALU.subtract, op1=ALU.mult,
             )
 
-        def gather_rows(b, a):
-            gate, drive = held["gate", b], held["drive", b]
+        def gather_rows(ch, a):
+            gate, drive = held["gate", ch], held["drive", ch]
             cols = slice(a * P, (a + 1) * P)
             x_acc = psum.tile([P, S], F32)
             terms = (gate[:, 0, :, cols], gate[:, 1, :, cols], drive[:, :, cols])
             for i, term in enumerate(terms):
                 for q in range(PLANES):
-                    scaled = (i, q) in TENSOR_GATES
+                    scaled = i == 1 and q in TENSOR_PLANES
                     nc.tensor.matmul(
                         out=x_acc[:, q * P : (q + 1) * P], lhsT=term[:, q, :],
                         rhs=gain_diag[:, q, :] if scaled else ident[:], is_transpose=not scaled,
                         start=(i == 0 and q == 0), stop=(i == len(terms) - 1 and q == PLANES - 1),
                     )
-            held["x_acc%d" % a, b] = x_acc
+            held["x_acc%d" % a, ch] = x_acc
 
-        def row_stats(b, a):
+        def row_stats(ch, a):
             stats = work.tile([P, 6], F32)
-            nc.vector.bn_stats(out=stats[:], in_=held["x_acc%d" % a, b][:])
-            held["stats", b] = stats
+            nc.vector.bn_stats(out=stats[:], in_=held["x_acc%d" % a, ch][:])
+            held["stats", ch] = stats
 
-        def row_mean(b, a):
+        def row_mean(ch, a):
             if a == 0:
                 mean_var = work.tile([P, ROW_TILES, 2], F32)
-                held["mean_var", b] = mean_var
-            nc.vector.bn_aggr(out=held["mean_var", b][:, a, :], in_=held["stats", b][:])
+                held["mean_var", ch] = mean_var
+            nc.vector.bn_aggr(out=held["mean_var", ch][:, a, :], in_=held["stats", ch][:])
 
-        def centre(b, a):
+        def centre(ch, a):
             if a == 0:
                 centred = work.tile([P, ROW_TILES, S], F32)
-                held["centred", b] = centred
+                held["centred", ch] = centred
             nc.vector.scalar_tensor_tensor(
-                out=held["centred", b][:, a, :], in0=held["x_acc%d" % a, b][:],
-                scalar=held["mean_var", b][:, a, 0:1], in1=gamma_planes[:],
+                out=held["centred", ch][:, a, :], in0=held["x_acc%d" % a, ch][:],
+                scalar=held["mean_var", ch][:, a, 0:1], in1=gamma_planes[:],
                 op0=ALU.subtract, op1=ALU.mult,
             )
 
-        def statistics(i, a, filler1, filler2):
-            run(row_stats, i, a)
-            if i == LAST:
-                last_shift_store(i - 1, a)
-            filler1()
-            run(row_mean, i, a)
-            filler2()
-            run(centre, i, a)
-            if i == LAST:
-                last_scale(i, a)
-                if a > 0:
-                    last_shift_store(i, a - 1)
+        def cell_order(tile, a):
+            return tile[:, a, :].rearrange("r (u j e) -> r u j e", u=2, e=2)
 
-        def inverse_std(b):
+        def plane_order(tile, a):
+            return tile[:, a, :].rearrange("r (u e j) -> r u j e", u=2, e=2)
+
+        def finish_on_gpsimd(ch):
             var_eps = work.tile([P, ROW_TILES], F32)
-            nc.gpsimd.tensor_scalar_add(out=var_eps[:], in0=held["mean_var", b][:, :, 1], scalar1=EPS)
+            nc.gpsimd.tensor_scalar_add(out=var_eps[:], in0=held["mean_var", ch][:, :, 1], scalar1=EPS)
             rstd = work.tile([P, ROW_TILES], F32)
             nc.gpsimd.tensor_tensor(out=rstd[:], in0=var_eps[:], in1=neg_half[:], op=ALU.pow)
-            held["rstd", b] = rstd
-
-        def scale_shift_store(b):
-            centred, rstd = held["centred", b], held["rstd", b]
             out_sb = work.tile([P, ROW_TILES, S], F32)
             for a in range(ROW_TILES):
                 nc.gpsimd.tensor_scalar(
-                    out=out_sb[:, a, :].rearrange("r (u j e) -> r u j e", u=2, e=2),
-                    in0=centred[:, a, :].rearrange("r (u e j) -> r u j e", u=2, e=2),
+                    out=cell_order(out_sb, a), in0=plane_order(held["centred", ch], a),
                     scalar1=rstd[:, a : a + 1], scalar2=0.0, op0=ALU.mult, op1=ALU.add,
                 )
             nc.gpsimd.tensor_tensor(
@@ -405,63 +387,74 @@ def tile_memorylayercell_pa_t_kernel(
                 op=ALU.add,
             )
             nc.sync.dma_start(
-                out=out[b * BLOCK : (b + 1) * BLOCK, :].rearrange("(p a) c -> p (a c)", a=ROW_TILES),
+                out=out[ch * CHUNK : (ch + 1) * CHUNK, :].rearrange("(p a) c -> p (a c)", a=ROW_TILES),
                 in_=out_sb[:].rearrange("p a c -> p (a c)"),
             )
 
-        def last_scale(b, a):
+        def late_scale(ch, a):
             if a == 0:
                 var_eps = work.tile([P, ROW_TILES], F32)
                 rstd = work.tile([P, ROW_TILES], F32)
                 out_sb = work.tile([P, ROW_TILES, S], F32)
-                held["var_eps", b], held["rstd", b], held["out_sb", b] = var_eps, rstd, out_sb
-            var_eps, rstd = held["var_eps", b], held["rstd", b]
+                held["var_eps", ch], held["rstd", ch], held["out_sb", ch] = var_eps, rstd, out_sb
+            var_eps, rstd = held["var_eps", ch], held["rstd", ch]
             nc.gpsimd.tensor_scalar_add(
-                out=var_eps[:, a : a + 1], in0=held["mean_var", b][:, a, 1:2], scalar1=EPS
+                out=var_eps[:, a : a + 1], in0=held["mean_var", ch][:, a, 1:2], scalar1=EPS
             )
             nc.gpsimd.tensor_tensor(
                 out=rstd[:, a : a + 1], in0=var_eps[:, a : a + 1], in1=neg_half[:, a : a + 1], op=ALU.pow
             )
             nc.scalar.activation(
-                out=held["out_sb", b][:, a, :].rearrange("r (u j e) -> r u j e", u=2, e=2),
-                in_=held["centred", b][:, a, :].rearrange("r (u e j) -> r u j e", u=2, e=2),
+                out=cell_order(held["out_sb", ch], a), in_=plane_order(held["centred", ch], a),
                 func=ACT.Identity, scale=rstd[:, a : a + 1],
             )
 
-        def last_shift_store(b, a):
-            out_sb = held["out_sb", b]
+        def late_shift_store(ch, a):
+            out_sb = held["out_sb", ch]
             nc.vector.tensor_tensor(out=out_sb[:, a, :], in0=out_sb[:, a, :], in1=beta_f32[:], op=ALU.add)
             nc.sync.dma_start(
-                out=out[b * BLOCK : (b + 1) * BLOCK, :].rearrange("(p a) c -> p a c", a=ROW_TILES)[:, a, :],
+                out=out[ch * CHUNK : (ch + 1) * CHUNK, :].rearrange("(p a) c -> p a c", a=ROW_TILES)[:, a, :],
                 in_=out_sb[:, a, :],
             )
 
-        for i in range(-3, N_BLOCKS):
+        def statistics(i, a, filler1, filler2):
+            run(row_stats, i, a)
+            if i == LAST:
+                late_shift_store(i - 1, a)
+            filler1()
+            run(row_mean, i, a)
+            filler2()
+            run(centre, i, a)
+            if i == LAST:
+                late_scale(i, a)
+                if a > 0:
+                    late_shift_store(i, a - 1)
+
+        for i in range(-3, N_CHUNKS):
             run(load, i + 4)
             run(drive_term, i)
             if i == LAST:
                 for a in range(ROW_TILES):
-                    last_scale(i - 1, a)
+                    late_scale(i - 1, a)
             else:
-                run(inverse_std, i - 1)
-                run(scale_shift_store, i - 1)
-            run(currents, i + 1, 1)
-            run(currents, i + 1, 2)
+                run(finish_on_gpsimd, i - 1)
+            run(current, i + 1, 0, 1)
+            run(current, i + 1, 1, 0)
             run(transpose_cat, i + 3, 0, 0)
             run(transpose_cat, i + 3, 0, 1)
             run(transpose_states, i + 1, 1)
             run(first_product, i + 1, 0)
             run(first_product, i + 1, 1)
             run(add_bias, i + 1, 0)
-            run(currents, i + 1, 3)
+            run(current, i + 1, 1, 1)
             run(add_bias, i + 1, 1)
-            run(currents, i + 1, 7)
+            run(current, i + 1, 3, 1)
             run(gates, i + 2, 0)
             run(gather_rows, i, 0)
             run(transpose_cat, i + 3, 1, 0)
             run(gather_rows, i, 1)
             run(transpose_cat, i + 3, 1, 1)
-            statistics(i, 0, lambda: run(currents, i + 1, 4), lambda: run(currents, i + 1, 5))
+            statistics(i, 0, lambda: run(current, i + 1, 2, 0), lambda: run(current, i + 1, 2, 1))
             run(gates, i + 2, 1)
             run(first_product, i + 1, 2)
             run(first_product, i + 1, 3)
@@ -469,7 +462,7 @@ def tile_memorylayercell_pa_t_kernel(
             run(gather_rows, i, 2)
             run(transpose_states, i + 2, 0)
             run(gather_rows, i, 3)
-            statistics(i, 2, lambda: run(quantise_h, i + 1), lambda: run(currents, i + 1, 6))
+            statistics(i, 2, lambda: run(quantise_h, i + 1), lambda: run(current, i + 1, 3, 0))
             run(second_product, i + 1)
-            statistics(i, 3, lambda: run(quantise_cat, i + 3), lambda: run(currents, i + 2, 0))
-        last_shift_store(LAST, 3)
+            statistics(i, 3, lambda: run(quantise_cat, i + 3), lambda: run(current, i + 2, 0, 0))
+        late_shift_store(LAST, 3)

from contextlib import ExitStack

import concourse.mybir as mybir
from concourse.masks import make_identity

F32 = mybir.dt.float32
BF16 = mybir.dt.bfloat16
U32 = mybir.dt.uint32
U8 = mybir.dt.uint8
FP8X4 = mybir.dt.float8_e4m3fn_x4
ALU = mybir.AluOpType
ACT = mybir.ActivationFunctionType

P = 128
PACK = 4
B, D, S = 8192, 512, 512
PAIRS = S // 2
EPS = 1e-6
ROW_TILES = 4
CHUNK = ROW_TILES * P
HALF = CHUNK // 2
N_CHUNKS = B // CHUNK
LAST = N_CHUNKS - 1
PLANES = 4
TENSOR_PLANES = (0, 1, 2)
GPSIMD_GATES = ((0, 0),)

FLOPS = 2 * B * ((D + S) * S + S * PAIRS)


def load_cell_constants(nc, pool, vectors, tables, b1, b2):
    slot = 16
    raw = pool.tile([P, 8, slot], BF16)
    nc.vector.memset(raw[:], 0.0)
    with nc.allow_non_contiguous_dma(reason="per-cell constants, a few bytes a partition, loaded once"):
        for i, vec in enumerate(vectors):
            nc.scalar.dma_start(
                out=raw[:, i, 0:PLANES].rearrange("p (u e) -> p u e", u=2),
                in_=vec.rearrange("(u p e) -> p u e", u=2, p=P),
            )
        for i, tab in enumerate(tables):
            nc.scalar.dma_start(
                out=raw[:, 3 + i, 0 : 2 * PLANES].rearrange("p (u k) -> p u k", u=2),
                in_=tab.rearrange("(u p e) c -> p u (e c)", u=2, p=P),
            )
        nc.scalar.dma_start(out=raw[:, 6, 0:2], in_=b2.rearrange("(u p) -> p u", p=P))
        nc.scalar.dma_start(out=raw[:, 7, 0:PACK], in_=b1.rearrange("(m t) -> m t", t=PACK))
    return raw


def tile_memorylayercell_pa_t_kernel(
    tc,
    inputs,
    states,
    W1,
    b1,
    W2,
    b2,
    excitatory_potential,
    inhibitory_potential,
    capacitance,
    max_conductance,
    mean_conductance_potential,
    std_conductance,
    gamma,
    beta,
    out,
):
    nc = tc.nc
    with ExitStack() as stack:
        consts = stack.enter_context(tc.tile_pool(name="consts", bufs=1))
        rows_in = stack.enter_context(tc.tile_pool(name="rows_in", bufs=3))
        work = stack.enter_context(tc.tile_pool(name="work", bufs=2))
        psum = stack.enter_context(tc.psum_pool(name="psum", bufs=2))
        stack.enter_context(tc.manual_schedule())
        held = {}

        def load(ch):
            rows = slice(ch * CHUNK, (ch + 1) * CHUNK)
            in_sb = rows_in.tile([P, ROW_TILES * D], BF16)
            nc.sync.dma_start(out=in_sb[:], in_=inputs[rows, :].rearrange("(p a) d -> p (a d)", a=ROW_TILES))
            st_sb = rows_in.tile([P, ROW_TILES * S], BF16, bufs=4)
            nc.sync.dma_start(out=st_sb[:], in_=states[rows, :].rearrange("(p a) d -> p (a d)", a=ROW_TILES))
            held["in_sb", ch] = in_sb
            held["st_sb", ch] = st_sb

        w1_raw = consts.tile([P, 2, PACK, S], BF16)
        nc.sync.dma_start(
            out=w1_raw[:].rearrange("p g (u e) n -> p (g u) (e n)", u=2),
            in_=W1.rearrange("(gu p e) n -> p gu (e n)", gu=4, p=P),
        )
        load(0)
        w2_raw = consts.tile([P, PACK, PAIRS], BF16)
        nc.sync.dma_start(
            out=w2_raw[:].rearrange("m t n -> m (t n)"),
            in_=W2.rearrange("(m t) n -> m (t n)", t=PACK),
        )
        raw = load_cell_constants(
            nc,
            consts,
            [excitatory_potential, inhibitory_potential, capacitance],
            [max_conductance, mean_conductance_potential, std_conductance],
            b1,
            b2,
        )
        gamma_rows = consts.tile([P, S], BF16)
        nc.scalar.dma_start(out=gamma_rows[:], in_=gamma.partition_broadcast(P))
        beta_rows = consts.tile([P, S], BF16)
        nc.scalar.dma_start(out=beta_rows[:], in_=beta.partition_broadcast(P))

        ident = consts.tile([P, P], F32)
        make_identity(nc, ident[:])

        w1_grp = consts.tile([P, 2, S * PACK], BF16, align_bytes=64)
        w1_codes = consts.tile([P, 2, S], U32, align_bytes=64)
        w1_scales = consts.tile([P, 2, S], U8, align_bytes=64)
        for g, copy in enumerate((nc.vector.tensor_copy, nc.scalar.copy)):
            copy(
                out=w1_grp[:, g, :].rearrange("p (c m t) -> p c m t", c=PACK, m=P),
                in_=w1_raw[:, g, :, :].rearrange("p t (m c) -> p c m t", c=PACK),
            )
        w2_grp = consts.tile([P, PAIRS, PACK], BF16, align_bytes=64)
        nc.vector.tensor_copy(out=w2_grp[:], in_=w2_raw[:].rearrange("m t n -> m n t"))
        for g in range(2):
            nc.vector.quantize_mx(
                out=w1_codes[:, g, :].bitcast(FP8X4), scales=w1_scales[:, g, :], in_=w1_grp[:, g, :]
            )
        w2_codes = consts.tile([P, PAIRS], U32, align_bytes=64)
        w2_scales = consts.tile([P, PAIRS], U8, align_bytes=64)
        nc.vector.quantize_mx(
            out=w2_codes[:].bitcast(FP8X4), scales=w2_scales[:], in_=w2_grp[:].rearrange("m n t -> m (n t)")
        )

        par = consts.tile([P, 8, 16], F32)
        nc.vector.tensor_copy(out=par[:], in_=raw[:])
        reversal = [par[:, 0, 0:PLANES], par[:, 1, 0:PLANES]]
        b1_col = par[:, 7, 0:PACK]
        inv_cap = consts.tile([P, PLANES], F32)
        nc.vector.reciprocal(out=inv_cap[:], in_=par[:, 2, 0:PLANES])
        slope = []
        shift = []
        neg_gain = []
        for k in range(2):
            slope_k = consts.tile([P, PLANES], F32, name="slope%d" % k)
            nc.vector.tensor_copy(out=slope_k[:], in_=par[:, 5, k : 2 * PLANES : 2])
            shift_k = consts.tile([P, PLANES], F32, name="shift%d" % k)
            nc.vector.scalar_tensor_tensor(
                out=shift_k[:], in0=slope_k[:], scalar=-1.0, in1=par[:, 4, k : 2 * PLANES : 2],
                op0=ALU.mult, op1=ALU.mult,
            )
            neg_gain_k = consts.tile([P, PLANES], F32, name="neg_gain%d" % k)
            nc.vector.scalar_tensor_tensor(
                out=neg_gain_k[:], in0=par[:, 3, k : 2 * PLANES : 2], scalar=-1.0, in1=inv_cap[:],
                op0=ALU.mult, op1=ALU.mult,
            )
            slope.append(slope_k)
            shift.append(shift_k)
            neg_gain.append(neg_gain_k)
        gain_diag = consts.tile([P, PLANES, P], F32)
        for q in TENSOR_PLANES:
            nc.vector.tensor_scalar_mul(out=gain_diag[:, q, :], in0=ident[:], scalar1=neg_gain[1][:, q : q + 1])
        gate_offset = consts.tile([P, 2], F32)
        nc.vector.memset(gate_offset[:, 0:1], 1.0)
        nc.vector.memset(gate_offset[:, 1:2], 0.0)
        drive_scale = consts.tile([P, PLANES], F32)
        nc.vector.tensor_copy(out=drive_scale[:, 0:PLANES:2], in_=inv_cap[:, 0:PLANES:2])
        nc.vector.tensor_scalar_mul(out=drive_scale[:, 1:PLANES:2], in0=inv_cap[:, 1:PLANES:2], scalar1=-1.0)
        drive_bias = consts.tile([P, PLANES], F32)
        nc.vector.tensor_mul(
            out=drive_bias[:].rearrange("p (u e) -> p u e", u=2),
            in0=drive_scale[:].rearrange("p (u e) -> p u e", u=2),
            in1=par[:, 6, 0:2].unsqueeze(2).to_broadcast([P, 2, 2]),
        )
        nc.vector.tensor_add(out=drive_bias[:], in0=drive_bias[:], in1=reversal[0])
        neg_half = consts.tile([P, ROW_TILES], F32)
        nc.vector.memset(neg_half[:], -0.5)
        gamma_planes = consts.tile([P, S], BF16)
        nc.vector.tensor_copy(
            out=gamma_planes[:].rearrange("r (u e j) -> r u e j", u=2, e=2),
            in_=gamma_rows[:].rearrange("r (u j e) -> r u e j", u=2, e=2),
        )
        beta_f32 = consts.tile([P, S], F32)
        nc.vector.tensor_copy(out=beta_f32[:], in_=beta_rows[:])

        def run(stage, ch, *args):
            if 0 <= ch < N_CHUNKS:
                stage(ch, *args)

        def transpose_cat(ch, g, half):
            if g == 0 and half == 0:
                cat_grp = work.tile([P, 2, CHUNK * PACK], BF16, align_bytes=64)
                held["cat_grp", ch] = cat_grp
            grp_words = held["cat_grp", ch][:, g, :].bitcast(F32).rearrange("p (r u) -> p r u", u=2)
            words = held[("in_sb", "st_sb")[g], ch][:].bitcast(F32).rearrange("p (a w) -> p a w", a=ROW_TILES)
            cat_t = psum.tile([P, 2, HALF], F32)
            for u in range(2):
                for al in range(2):
                    nc.tensor.transpose(
                        out=cat_t[:, u, al * P : (al + 1) * P],
                        in_=words[:, 2 * half + al, u * P : (u + 1) * P],
                        identity=ident[:],
                    )
            nc.scalar.copy(
                out=grp_words[:, half * HALF : (half + 1) * HALF, :],
                in_=cat_t[:].rearrange("p u r -> p r u"),
            )

        def quantise_cat(ch):
            cat_codes = work.tile([P, 2, CHUNK], U32, align_bytes=64)
            cat_scales = work.tile([P, 2, CHUNK], U8, align_bytes=64)
            nc.vector.quantize_mx(
                out=cat_codes[:].rearrange("p g r -> p (g r)").bitcast(FP8X4),
                scales=cat_scales[:].rearrange("p g r -> p (g r)"),
                in_=held["cat_grp", ch][:].rearrange("p g c -> p (g c)"),
            )
            held["cat_codes", ch] = cat_codes
            held["cat_scales", ch] = cat_scales

        def first_product(ch, a):
            cat_codes, cat_scales = held["cat_codes", ch], held["cat_scales", ch]
            cols = slice(a * P, (a + 1) * P)
            h_acc = psum.tile([P, PACK, P], F32, tag="mx_acc")
            held["h_acc%d" % a, ch] = h_acc
            for c in range(PACK):
                for g in range(2):
                    nc.tensor.matmul_mx(
                        out=h_acc[:, c, :],
                        lhsT=w1_codes[:, g, c * P : (c + 1) * P].bitcast(FP8X4),
                        lhsT_scale=w1_scales[:, g, c * P : (c + 1) * P],
                        rhs=cat_codes[:, g, cols].bitcast(FP8X4),
                        rhs_scale=cat_scales[:, g, cols],
                        start=(g == 0),
                        stop=(g == 1),
                    )

        def add_bias(ch, a):
            if a == 0:
                h_grp = work.tile([P, CHUNK, PACK], BF16, align_bytes=64)
                held["h_grp", ch] = h_grp
            nc.vector.tensor_tensor(
                out=held["h_grp", ch][:, a * P : (a + 1) * P, :],
                in0=held["h_acc%d" % a, ch][:].rearrange("m c r -> m r c"),
                in1=b1_col.unsqueeze(1).to_broadcast([P, P, PACK]),
                op=ALU.add,
            )

        def quantise_h(ch):
            h_codes = work.tile([P, CHUNK], U32, align_bytes=64)
            h_scales = work.tile([P, CHUNK], U8, align_bytes=64)
            nc.vector.quantize_mx(
                out=h_codes[:].bitcast(FP8X4), scales=h_scales[:],
                in_=held["h_grp", ch][:].rearrange("m r c -> m (r c)"),
            )
            held["h_codes", ch] = h_codes
            held["h_scales", ch] = h_scales

        def second_product(ch):
            for u in range(2):
                pre_acc = psum.tile([P, CHUNK], F32, tag="mx_acc")
                nc.tensor.matmul_mx(
                    out=pre_acc[:],
                    lhsT=w2_codes[:, u * P : (u + 1) * P].bitcast(FP8X4),
                    lhsT_scale=w2_scales[:, u * P : (u + 1) * P],
                    rhs=held["h_codes", ch][:].bitcast(FP8X4),
                    rhs_scale=held["h_scales", ch][:],
                    start=True,
                    stop=True,
                )
                held["pre_acc%d" % u, ch] = pre_acc

        def drive_term(ch):
            drive = work.tile([P, PLANES, CHUNK], F32)
            for q in range(PLANES):
                nc.scalar.activation(
                    out=drive[:, q, :], in_=held["pre_acc%d" % (q // 2), ch][:], func=ACT.Identity,
                    scale=drive_scale[:, q : q + 1], bias=drive_bias[:, q : q + 1],
                )
            held["drive", ch] = drive

        def gates(ch, u):
            v = held["cat_grp", ch][:, 1, :].rearrange("p (r q) -> p r q", q=PLANES)
            if u == 0:
                gate = work.tile([P, 2, PLANES, CHUNK], F32, bufs=3)
                held["gate", ch] = gate
            gate = held["gate", ch]

            def scale_on_scalar(k, q):
                nc.scalar.activation(
                    out=gate[:, k, q, :], in_=gate[:, k, q, :], func=ACT.Identity,
                    scale=neg_gain[k][:, q : q + 1], bias=gate_offset[:, k : k + 1],
                )

            owed = None
            for k, q in ((1, 2 * u), (0, 2 * u), (1, 2 * u + 1), (0, 2 * u + 1)):
                seen = q if k == 0 else q ^ 1
                nc.scalar.activation(
                    out=gate[:, k, q, :], in_=v[:, :, seen], func=ACT.Sigmoid,
                    scale=slope[k][:, q : q + 1], bias=shift[k][:, q : q + 1],
                )
                if owed is not None:
                    scale_on_scalar(owed[0], owed[1])
                owed = None
                if (k, q) in GPSIMD_GATES:
                    nc.gpsimd.tensor_scalar(
                        out=gate[:, k, q, :], in0=gate[:, k, q, :],
                        scalar1=neg_gain[k][:, q : q + 1], scalar2=gate_offset[:, k : k + 1],
                        op0=ALU.mult, op1=ALU.add,
                    )
                elif k == 0 or q not in TENSOR_PLANES:
                    owed = (k, q)
            if owed is not None:
                scale_on_scalar(owed[0], owed[1])

        def transpose_states(ch, u):
            st_v = psum.tile([P, CHUNK], F32)
            words = held["st_sb", ch][:].bitcast(F32).rearrange("p (a w) -> p a w", a=ROW_TILES)
            for a in range(ROW_TILES):
                nc.tensor.transpose(
                    out=st_v[:, a * P : (a + 1) * P], in_=words[:, a, u * P : (u + 1) * P], identity=ident[:]
                )
            held["st_v%d" % u, ch] = st_v

        def current(ch, q, k):
            gate = held["gate", ch]
            v_psum = held["st_v%d" % (q // 2), ch][:].bitcast(BF16).rearrange("p (r e) -> p r e", e=2)
            nc.vector.scalar_tensor_tensor(
                out=gate[:, k, q, :], in0=v_psum[:, :, q % 2],
                scalar=reversal[k][:, q : q + 1], in1=gate[:, k, q, :],
                op0=ALU.subtract, op1=ALU.mult,
            )

        def gather_rows(ch, a):
            gate, drive = held["gate", ch], held["drive", ch]
            cols = slice(a * P, (a + 1) * P)
            x_acc = psum.tile([P, S], F32)
            terms = (gate[:, 0, :, cols], gate[:, 1, :, cols], drive[:, :, cols])
            for i, term in enumerate(terms):
                for q in range(PLANES):
                    scaled = i == 1 and q in TENSOR_PLANES
                    nc.tensor.matmul(
                        out=x_acc[:, q * P : (q + 1) * P], lhsT=term[:, q, :],
                        rhs=gain_diag[:, q, :] if scaled else ident[:], is_transpose=not scaled,
                        start=(i == 0 and q == 0), stop=(i == len(terms) - 1 and q == PLANES - 1),
                    )
            held["x_acc%d" % a, ch] = x_acc

        def row_stats(ch, a):
            stats = work.tile([P, 6], F32)
            nc.vector.bn_stats(out=stats[:], in_=held["x_acc%d" % a, ch][:])
            held["stats", ch] = stats

        def row_mean(ch, a):
            if a == 0:
                mean_var = work.tile([P, ROW_TILES, 2], F32)
                held["mean_var", ch] = mean_var
            nc.vector.bn_aggr(out=held["mean_var", ch][:, a, :], in_=held["stats", ch][:])

        def centre(ch, a):
            if a == 0:
                centred = work.tile([P, ROW_TILES, S], F32)
                held["centred", ch] = centred
            nc.vector.scalar_tensor_tensor(
                out=held["centred", ch][:, a, :], in0=held["x_acc%d" % a, ch][:],
                scalar=held["mean_var", ch][:, a, 0:1], in1=gamma_planes[:],
                op0=ALU.subtract, op1=ALU.mult,
            )

        def cell_order(tile, a):
            return tile[:, a, :].rearrange("r (u j e) -> r u j e", u=2, e=2)

        def plane_order(tile, a):
            return tile[:, a, :].rearrange("r (u e j) -> r u j e", u=2, e=2)

        def finish_on_gpsimd(ch):
            var_eps = work.tile([P, ROW_TILES], F32)
            nc.gpsimd.tensor_scalar_add(out=var_eps[:], in0=held["mean_var", ch][:, :, 1], scalar1=EPS)
            rstd = work.tile([P, ROW_TILES], F32)
            nc.gpsimd.tensor_tensor(out=rstd[:], in0=var_eps[:], in1=neg_half[:], op=ALU.pow)
            out_sb = work.tile([P, ROW_TILES, S], F32)
            for a in range(ROW_TILES):
                nc.gpsimd.tensor_scalar(
                    out=cell_order(out_sb, a), in0=plane_order(held["centred", ch], a),
                    scalar1=rstd[:, a : a + 1], scalar2=0.0, op0=ALU.mult, op1=ALU.add,
                )
            nc.gpsimd.tensor_tensor(
                out=out_sb[:], in0=out_sb[:], in1=beta_f32[:].unsqueeze(1).to_broadcast([P, ROW_TILES, S]),
                op=ALU.add,
            )
            nc.sync.dma_start(
                out=out[ch * CHUNK : (ch + 1) * CHUNK, :].rearrange("(p a) c -> p (a c)", a=ROW_TILES),
                in_=out_sb[:].rearrange("p a c -> p (a c)"),
            )

        def late_scale(ch, a):
            if a == 0:
                var_eps = work.tile([P, ROW_TILES], F32)
                rstd = work.tile([P, ROW_TILES], F32)
                out_sb = work.tile([P, ROW_TILES, S], F32)
                held["var_eps", ch], held["rstd", ch], held["out_sb", ch] = var_eps, rstd, out_sb
            var_eps, rstd = held["var_eps", ch], held["rstd", ch]
            nc.gpsimd.tensor_scalar_add(
                out=var_eps[:, a : a + 1], in0=held["mean_var", ch][:, a, 1:2], scalar1=EPS
            )
            nc.gpsimd.tensor_tensor(
                out=rstd[:, a : a + 1], in0=var_eps[:, a : a + 1], in1=neg_half[:, a : a + 1], op=ALU.pow
            )
            nc.scalar.activation(
                out=cell_order(held["out_sb", ch], a), in_=plane_order(held["centred", ch], a),
                func=ACT.Identity, scale=rstd[:, a : a + 1],
            )

        def late_shift_store(ch, a):
            out_sb = held["out_sb", ch]
            nc.vector.tensor_tensor(out=out_sb[:, a, :], in0=out_sb[:, a, :], in1=beta_f32[:], op=ALU.add)
            nc.sync.dma_start(
                out=out[ch * CHUNK : (ch + 1) * CHUNK, :].rearrange("(p a) c -> p a c", a=ROW_TILES)[:, a, :],
                in_=out_sb[:, a, :],
            )

        def statistics(i, a, filler1, filler2):
            run(row_stats, i, a)
            if i == LAST:
                late_shift_store(i - 1, a)
            filler1()
            run(row_mean, i, a)
            filler2()
            run(centre, i, a)
            if i == LAST:
                late_scale(i, a)
                if a > 0:
                    late_shift_store(i, a - 1)

        for i in range(-3, N_CHUNKS):
            run(load, i + 4)
            run(drive_term, i)
            if i == LAST:
                for a in range(ROW_TILES):
                    late_scale(i - 1, a)
            else:
                run(finish_on_gpsimd, i - 1)
            run(current, i + 1, 0, 1)
            run(current, i + 1, 1, 0)
            run(transpose_cat, i + 3, 0, 0)
            run(transpose_cat, i + 3, 0, 1)
            run(transpose_states, i + 1, 1)
            run(first_product, i + 1, 0)
            run(first_product, i + 1, 1)
            run(add_bias, i + 1, 0)
            run(current, i + 1, 1, 1)
            run(add_bias, i + 1, 1)
            run(current, i + 1, 3, 1)
            run(gates, i + 2, 0)
            run(gather_rows, i, 0)
            run(transpose_cat, i + 3, 1, 0)
            run(gather_rows, i, 1)
            run(transpose_cat, i + 3, 1, 1)
            statistics(i, 0, lambda: run(current, i + 1, 2, 0), lambda: run(current, i + 1, 2, 1))
            run(gates, i + 2, 1)
            run(first_product, i + 1, 2)
            run(first_product, i + 1, 3)
            statistics(i, 1, lambda: run(add_bias, i + 1, 2), lambda: run(add_bias, i + 1, 3))
            run(gather_rows, i, 2)
            run(transpose_states, i + 2, 0)
            run(gather_rows, i, 3)
            statistics(i, 2, lambda: run(quantise_h, i + 1), lambda: run(current, i + 1, 3, 0))
            run(second_product, i + 1)
            statistics(i, 3, lambda: run(quantise_cat, i + 3), lambda: run(current, i + 2, 0, 0))
        late_shift_store(LAST, 3)
